import numpy as np
import ml_dtypes


def mxq(x, axis, fmt="e4m3"):
    dtype, down = {"e4m3": (ml_dtypes.float8_e4m3fn, 7), "e5m2": (ml_dtypes.float8_e5m2, 14)}[fmt]
    v = np.moveaxis(np.asarray(x, np.float32).astype(ml_dtypes.bfloat16).astype(np.float64), axis, -1)
    blocks = v.reshape(v.shape[:-1] + (-1, 32))
    amax = np.abs(blocks).max(-1, keepdims=True)
    byte = np.maximum(np.where(amax > 0, np.frexp(amax)[1] - 1 + 127, 0) - down, 1)
    scale = np.exp2(byte - 127.0)
    codes = (blocks / scale).astype(np.float32).astype(dtype).astype(np.float64)
    return np.moveaxis((codes * scale).reshape(v.shape), -1, axis)


WIDE = False


def mx_kscale(k):
    if not WIDE:
        return np.ones(k)
    levels = np.array([10, -10, 5, -5, 0])
    a = np.random.permutation(np.resize(levels, k // 512 * 4)).reshape(k // 512, 4)
    idx = np.arange(k)
    return np.exp2(a[idx // 512, idx % 128 // 32])


BF16 = ml_dtypes.bfloat16


def bf(x):
    return np.asarray(x, np.float32).astype(BF16)


def f64(x):
    return np.asarray(x).astype(np.float64)


E2M1 = np.array([0.0, 0.5, 1.0, 1.5, 2.0, 3.0, 4.0, 6.0, -0.0, -0.5, -1.0, -1.5, -2.0, -3.0, -4.0, -6.0])


def pack_weight(w, fmt):
    k, n = w.shape
    w = f64(bf(w)).reshape(k // 32, 32, n)
    amax = np.abs(w).max(1)
    if fmt == "e4m3":
        byte = np.frexp(amax)[1] - 1 + 127 - 7
    else:
        mant, ex = np.frexp(amax / 6.0)
        byte = np.where(mant > 0.5, ex, ex - 1) + 127
    byte = np.clip(np.where(amax > 0, byte, 1), 1, 254)
    scaled = (w * np.exp2(127.0 - byte)[:, None, :]).reshape(k, n).astype(np.float32)
    by_word = np.ascontiguousarray(scaled.reshape(k // 512, 128, 4, n).transpose(0, 1, 3, 2))
    if fmt == "e4m3":
        words = by_word.astype(ml_dtypes.float8_e4m3fn).view(np.uint8)
    else:
        c = by_word.astype(ml_dtypes.float4_e2m1fn).view(np.uint8) & 0xF
        words = c[..., 0::2] | (c[..., 1::2] << 4)
    return np.ascontiguousarray(words), np.ascontiguousarray(byte.astype(np.uint8).reshape(k // 512, 16, n))


def unpack_weight(words, scales, fmt):
    g, p, n, _ = words.shape
    if fmt == "e4m3":
        vals = np.ascontiguousarray(words).view(ml_dtypes.float8_e4m3fn).astype(np.float64)
    else:
        nib = np.empty((g, p, n, 4), np.uint8)
        nib[..., 0::2] = words & 0xF
        nib[..., 1::2] = words >> 4
        vals = E2M1[nib]
    vals = vals * np.repeat(np.exp2(scales.astype(np.float64) - 127.0), 8, axis=1)[..., None]
    return vals.transpose(0, 1, 3, 2).reshape(g * 512, n)

def pack4(w):
    words, scales = pack_weight(w, "e2m1")
    return words.reshape(words.shape[0], 128, -1), scales


def unpack4(words, scales):
    return unpack_weight(words.reshape(words.shape[0], 128, -1, 2), scales, "e2m1")


B, N, D, H, DK, DV = 4, 4096, 512, 4, 64, 64


def xnorm(x, g):
    n = np.sqrt(np.sum(x * x, axis=-1, keepdims=True))
    return x * g / n


def setup_inputs():
    s = mx_kscale(D)
    queries = bf(np.random.standard_normal((B, N, D)) * s)
    Wq_words, Wq_scales = pack4(np.random.standard_normal((D, H * DK)) / np.sqrt(D) / s[:, None])
    return {
        "queries": queries,
        "Wq_words": Wq_words,
        "Wq_scales": Wq_scales,
        "bq": bf(np.random.standard_normal(H * DK) * 0.1),
        "gamma": bf(np.random.standard_normal((1, H, 1, 1)) * 2.0),
    }


def reference(queries, Wq_words, Wq_scales, bq, gamma):
    q = ((mxq(f64(queries), 2, "e4m3") @ unpack4(Wq_words, Wq_scales)) + f64(bq)).reshape(B, N, H, DK)
    return xnorm(q.transpose(0, 2, 1, 3), f64(gamma))

@@ -1,0 +1,201 @@
+from contextlib import ExitStack
+
+import concourse.mybir as mybir
+from concourse.masks import make_identity
+
+F32 = mybir.dt.float32
+BF16 = mybir.dt.bfloat16
+I32 = mybir.dt.int32
+U32 = mybir.dt.uint32
+U8 = mybir.dt.uint8
+FP8X4 = mybir.dt.float8_e4m3fn_x4
+FP4X4 = mybir.dt.float4_e2m1fn_x4
+ADD = mybir.AluOpType.add
+MULT = mybir.AluOpType.mult
+SQUARE = mybir.ActivationFunctionType.Square
+SQRT = mybir.ActivationFunctionType.Sqrt
+
+P = 128
+BATCH, TOKENS, K = 4, 4096, 512
+HEADS, HEAD_DIM = 4, 64
+FEATURES = HEADS * HEAD_DIM
+WORDS = K // 2
+SUB = 8
+CHUNK = P * SUB
+CHUNKS_PER_BATCH = TOKENS // CHUNK
+N_CHUNKS = BATCH * CHUNKS_PER_BATCH
+PER_BANK = 2
+BANKS = SUB // PER_BANK
+AHEAD = 3
+
+FLOPS = 2 * BATCH * TOKENS * K * FEATURES
+
+
+def tile_ufoattention_pb_t_kernel(tc, queries, Wq_words, Wq_scales, bq, gamma, out):
+    nc = tc.nc
+    with ExitStack() as ctx:
+        ctx.enter_context(tc.manual_schedule())
+        consts = ctx.enter_context(tc.tile_pool(name="consts", bufs=1))
+        x_pool = ctx.enter_context(tc.tile_pool(name="x", bufs=AHEAD + 1))
+        grouped_pool = ctx.enter_context(tc.tile_pool(name="grouped", bufs=2))
+        mx_pool = ctx.enter_context(tc.tile_pool(name="mx", bufs=2))
+        q_pool = ctx.enter_context(tc.tile_pool(name="q", bufs=4))
+        squares_pool = ctx.enter_context(tc.tile_pool(name="squares", bufs=2))
+        stats_pool = ctx.enter_context(tc.tile_pool(name="stats", bufs=3))
+        xt_pool = ctx.enter_context(tc.psum_pool(name="xt", bufs=BANKS))
+        y_pool = ctx.enter_context(tc.psum_pool(name="y", bufs=BANKS))
+
+        x_tiles, grouped_tiles, code_tiles, plane_tiles = {}, {}, {}, {}
+        y_tiles, q_tiles, norm_tiles = {}, {}, {}
+
+        def load(c):
+            batch, part = divmod(c, CHUNKS_PER_BATCH)
+            x_sb = x_pool.tile([P, SUB * K], BF16)
+            rows = queries[batch, part * CHUNK : (part + 1) * CHUNK, :]
+            nc.sync.dma_start(out=x_sb[:], in_=rows.rearrange("(p j) k -> p (j k)", j=SUB))
+            x_tiles[c] = x_sb
+
+        load(0)
+
+        w_words = consts.tile([P, 2 * FEATURES], U8, align_bytes=64)
+        nc.sync.dma_start(out=w_words[:].bitcast(I32), in_=Wq_words[0].bitcast(I32))
+        w_scales = consts.tile([P, FEATURES], U8, align_bytes=64)
+        nc.vector.memset(w_scales[:].bitcast(I32), 0)
+        for quad in range(4):
+            nc.sync.dma_start(
+                out=w_scales[32 * quad : 32 * quad + 4, :].bitcast(I32),
+                in_=Wq_scales[0, 4 * quad : 4 * quad + 4, :].bitcast(I32),
+            )
+        for c in range(1, AHEAD):
+            load(c)
+
+        one = consts.tile([P, 1], F32)
+        nc.vector.memset(one[:], 1.0)
+        nc.scalar.activation(out=one[:], in_=one[:], func=SQRT)
+
+        ident = consts.tile([P, P], F32)
+        make_identity(nc, ident[:])
+
+        vectors = consts.tile([P, PER_BANK * FEATURES], BF16)
+        nc.vector.memset(vectors[:], 0.0)
+        nc.scalar.dma_start(out=vectors[0:1, 0:FEATURES], in_=bq.rearrange("(a n) -> a n", a=1))
+        nc.scalar.dma_start(
+            out=vectors[0:1, FEATURES : FEATURES + HEADS],
+            in_=gamma.rearrange("a h b c -> a (h b c)"),
+        )
+        ones = consts.tile([P, P], BF16)
+        nc.vector.memset(ones[:], 1.0)
+        spread = y_pool.tile([P, PER_BANK, FEATURES], F32, tag="y_ps")
+        nc.tensor.matmul(
+            out=spread[:].rearrange("p a n -> p (a n)"), lhsT=ones[:], rhs=vectors[:], start=True, stop=True
+        )
+        bias = consts.tile([P, PER_BANK, FEATURES], F32)
+        nc.vector.tensor_copy(
+            out=bias[:], in_=spread[:, 0:1, :].to_broadcast([P, PER_BANK, FEATURES])
+        )
+        gain = consts.tile([P, HEADS], F32)
+        nc.vector.tensor_copy(out=gain[:], in_=spread[:, 1, 0:HEADS])
+
+        def transpose_and_group(c):
+            x_words = x_tiles[c][:].bitcast(F32)
+            grouped = grouped_pool.tile([P, SUB * P * 4], BF16, align_bytes=64)
+            grouped_words = grouped[:].bitcast(F32).rearrange("p (j c u) -> p j c u", j=SUB, u=2)
+            for bank in range(BANKS):
+                xt = xt_pool.tile([P, PER_BANK, 2, P], F32)
+                for i in range(PER_BANK):
+                    j = bank * PER_BANK + i
+                    for u in range(2):
+                        nc.tensor.transpose(
+                            xt[:, i, u, :], x_words[:, j * WORDS + u : (j + 1) * WORDS : 2], ident[:]
+                        )
+                nc.scalar.copy(
+                    out=grouped_words[:, bank * PER_BANK : (bank + 1) * PER_BANK, :, :],
+                    in_=xt[:].rearrange("p i u c -> p i c u"),
+                )
+            grouped_tiles[c] = grouped
+
+        def quantise(c):
+            codes = mx_pool.tile([P, CHUNK], U32, align_bytes=64)
+            planes = mx_pool.tile([P, CHUNK], U8, align_bytes=64)
+            nc.vector.quantize_mx(
+                out=codes[:].bitcast(FP8X4), scales=planes[:], in_=grouped_tiles[c][:]
+            )
+            code_tiles[c], plane_tiles[c] = codes, planes
+
+        def project(c):
+            codes, planes = code_tiles[c], plane_tiles[c]
+            y_tiles[c] = []
+            for bank in range(BANKS):
+                y_ps = y_pool.tile([P, PER_BANK, FEATURES], F32)
+                for i in range(PER_BANK):
+                    cols = slice((bank * PER_BANK + i) * P, (bank * PER_BANK + i + 1) * P)
+                    nc.tensor.matmul_mx(
+                        out=y_ps[:, i, :],
+                        lhsT=codes[:, cols].bitcast(FP8X4),
+                        lhsT_scale=planes[:, cols],
+                        rhs=w_words[:].bitcast(FP4X4),
+                        rhs_scale=w_scales[:],
+                        start=True,
+                        stop=True,
+                    )
+                y_tiles[c].append(y_ps)
+
+        def add_bias(c):
+            q_sb = q_pool.tile([P, HEADS, SUB, HEAD_DIM], F32)
+            for bank, y_ps in enumerate(y_tiles[c]):
+                nc.vector.tensor_tensor(
+                    out=q_sb[:, :, bank * PER_BANK : (bank + 1) * PER_BANK, :].rearrange("p h i d -> p i h d"),
+                    in0=y_ps[:].rearrange("p i (h d) -> p i h d", h=HEADS),
+                    in1=bias[:].rearrange("p i (h d) -> p i h d", h=HEADS),
+                    op=ADD,
+                )
+            q_tiles[c] = q_sb
+
+        def norms(c):
+            q_sb = q_tiles[c]
+            squares = squares_pool.tile([P, HEADS, SUB, HEAD_DIM], F32)
+            sums = stats_pool.tile([P, HEADS, SUB], F32)
+            for h in range(HEADS):
+                for j in range(SUB):
+                    nc.scalar.activation(
+                        out=squares[:, h, j, :], in_=q_sb[:, h, j, :], func=SQUARE, accum_out=sums[:, h, j : j + 1]
+                    )
+            norm = stats_pool.tile([P, HEADS, SUB], F32)
+            nc.scalar.activation(out=norm[:], in_=sums[:], func=SQRT)
+            norm_tiles[c] = norm
+
+        def scale_and_store(c):
+            batch, part = divmod(c, CHUNKS_PER_BATCH)
+            q_sb, norm = q_tiles[c], norm_tiles[c]
+            factor = stats_pool.tile([P, HEADS, SUB], F32)
+            nc.vector.reciprocal(out=factor[:], in_=norm[:])
+            nc.vector.tensor_tensor(
+                out=factor[:], in0=factor[:], in1=gain[:].unsqueeze(2).to_broadcast([P, HEADS, SUB]), op=MULT
+            )
+            q_rows = q_sb[:].rearrange("p h j d -> p (h j) d")
+            nc.vector.tensor_tensor(
+                out=q_rows,
+                in0=q_rows,
+                in1=factor[:].rearrange("p h j -> p (h j)").unsqueeze(2).to_broadcast([P, HEADS * SUB, HEAD_DIM]),
+                op=MULT,
+            )
+            rows = out[batch, :, part * CHUNK : (part + 1) * CHUNK, :]
+            nc.sync.dma_start(
+                out=rows.rearrange("h (p j) d -> p h (j d)", j=SUB), in_=q_sb[:].rearrange("p h j d -> p h (j d)")
+            )
+
+        for s in range(N_CHUNKS + 3):
+            if s + AHEAD < N_CHUNKS:
+                load(s + AHEAD)
+            if 0 <= s - 1 < N_CHUNKS:
+                quantise(s - 1)
+            if s < N_CHUNKS:
+                transpose_and_group(s)
+            if 0 <= s - 1 < N_CHUNKS:
+                project(s - 1)
+            if 0 <= s - 3:
+                scale_and_store(s - 3)
+            if 0 <= s - 1 < N_CHUNKS:
+                add_bias(s - 1)
+            if 0 <= s - 2 < N_CHUNKS:
+                norms(s - 2)

@@ -27,6 +27,7 @@ N_CHUNKS = BATCH * CHUNKS_PER_BATCH
 PER_BANK = 2
 BANKS = SUB // PER_BANK
 AHEAD = 3
+GPSIMD_HEADS = 3
 
 FLOPS = 2 * BATCH * TOKENS * K * FEATURES
 
@@ -39,7 +40,7 @@ def tile_ufoattention_pb_t_kernel(tc, queries, Wq_words, Wq_scales, bq, gamma, o
         x_pool = ctx.enter_context(tc.tile_pool(name="x", bufs=AHEAD + 1))
         grouped_pool = ctx.enter_context(tc.tile_pool(name="grouped", bufs=2))
         mx_pool = ctx.enter_context(tc.tile_pool(name="mx", bufs=2))
-        q_pool = ctx.enter_context(tc.tile_pool(name="q", bufs=4))
+        q_pool = ctx.enter_context(tc.tile_pool(name="q", bufs=5))
         squares_pool = ctx.enter_context(tc.tile_pool(name="squares", bufs=2))
         stats_pool = ctx.enter_context(tc.tile_pool(name="stats", bufs=3))
         xt_pool = ctx.enter_context(tc.psum_pool(name="xt", bufs=BANKS))
@@ -108,10 +109,11 @@ def tile_ufoattention_pb_t_kernel(tc, queries, Wq_words, Wq_scales, bq, gamma, o
                         nc.tensor.transpose(
                             xt[:, i, u, :], x_words[:, j * WORDS + u : (j + 1) * WORDS : 2], ident[:]
                         )
-                nc.scalar.copy(
-                    out=grouped_words[:, bank * PER_BANK : (bank + 1) * PER_BANK, :, :],
-                    in_=xt[:].rearrange("p i u c -> p i c u"),
-                )
+                grouped_part = grouped_words[:, bank * PER_BANK : (bank + 1) * PER_BANK, :, :]
+                if bank % 2 == 0:
+                    nc.scalar.copy(out=grouped_part, in_=xt[:].rearrange("p i u c -> p i c u"))
+                else:
+                    nc.vector.tensor_copy(out=grouped_part, in_=xt[:].rearrange("p i u c -> p i c u"))
             grouped_tiles[c] = grouped
 
         def quantise(c):
@@ -172,13 +174,14 @@ def tile_ufoattention_pb_t_kernel(tc, queries, Wq_words, Wq_scales, bq, gamma, o
             nc.vector.tensor_tensor(
                 out=factor[:], in0=factor[:], in1=gain[:].unsqueeze(2).to_broadcast([P, HEADS, SUB]), op=MULT
             )
-            q_rows = q_sb[:].rearrange("p h j d -> p (h j) d")
-            nc.vector.tensor_tensor(
-                out=q_rows,
-                in0=q_rows,
-                in1=factor[:].rearrange("p h j -> p (h j)").unsqueeze(2).to_broadcast([P, HEADS * SUB, HEAD_DIM]),
-                op=MULT,
-            )
+            for h in range(HEADS):
+                engine = nc.gpsimd if h < GPSIMD_HEADS else nc.vector
+                engine.tensor_tensor(
+                    out=q_sb[:, h, :, :],
+                    in0=q_sb[:, h, :, :],
+                    in1=factor[:, h, :].unsqueeze(2).to_broadcast([P, SUB, HEAD_DIM]),
+                    op=MULT,
+                )
             rows = out[batch, :, part * CHUNK : (part + 1) * CHUNK, :]
             nc.sync.dma_start(
                 out=rows.rearrange("h (p j) d -> p h (j d)", j=SUB), in_=q_sb[:].rearrange("p h j d -> p h (j d)")

@@ -13,7 +13,7 @@ FP4X4 = mybir.dt.float4_e2m1fn_x4
 ADD = mybir.AluOpType.add
 MULT = mybir.AluOpType.mult
 SQUARE = mybir.ActivationFunctionType.Square
-SQRT = mybir.ActivationFunctionType.Sqrt
+RSQRT = mybir.ActivationFunctionType.Abs_reciprocal_sqrt
 
 P = 128
 BATCH, TOKENS, K = 4, 4096, 512
@@ -27,7 +27,7 @@ N_CHUNKS = BATCH * CHUNKS_PER_BATCH
 PER_BANK = 2
 BANKS = SUB // PER_BANK
 AHEAD = 3
-GPSIMD_HEADS = 3
+FIRST_LOAD_PIECES = 2
 
 FLOPS = 2 * BATCH * TOKENS * K * FEATURES
 
@@ -40,23 +40,26 @@ def tile_ufoattention_pb_t_kernel(tc, queries, Wq_words, Wq_scales, bq, gamma, o
         x_pool = ctx.enter_context(tc.tile_pool(name="x", bufs=AHEAD + 1))
         grouped_pool = ctx.enter_context(tc.tile_pool(name="grouped", bufs=2))
         mx_pool = ctx.enter_context(tc.tile_pool(name="mx", bufs=2))
-        q_pool = ctx.enter_context(tc.tile_pool(name="q", bufs=5))
+        q_pool = ctx.enter_context(tc.tile_pool(name="q", bufs=6))
         squares_pool = ctx.enter_context(tc.tile_pool(name="squares", bufs=2))
         stats_pool = ctx.enter_context(tc.tile_pool(name="stats", bufs=3))
         xt_pool = ctx.enter_context(tc.psum_pool(name="xt", bufs=BANKS))
         y_pool = ctx.enter_context(tc.psum_pool(name="y", bufs=BANKS))
 
         x_tiles, grouped_tiles, code_tiles, plane_tiles = {}, {}, {}, {}
-        y_tiles, q_tiles, norm_tiles = {}, {}, {}
+        y_tiles, q_tiles, sum_tiles, inverse_tiles = {}, {}, {}, {}
 
-        def load(c):
+        def load(c, pieces=1):
             batch, part = divmod(c, CHUNKS_PER_BATCH)
             x_sb = x_pool.tile([P, SUB * K], BF16)
-            rows = queries[batch, part * CHUNK : (part + 1) * CHUNK, :]
-            nc.sync.dma_start(out=x_sb[:], in_=rows.rearrange("(p j) k -> p (j k)", j=SUB))
+            rows = queries[batch, part * CHUNK : (part + 1) * CHUNK, :].rearrange("(p j) k -> p (j k)", j=SUB)
+            width = SUB * K // pieces
+            for i in range(pieces):
+                nc.sync.dma_start(out=x_sb[:, i * width : (i + 1) * width], in_=rows[:, i * width : (i + 1) * width])
             x_tiles[c] = x_sb
 
-        load(0)
+        load(0, pieces=FIRST_LOAD_PIECES)
+        load(1)
 
         w_words = consts.tile([P, 2 * FEATURES], U8, align_bytes=64)
         nc.sync.dma_start(out=w_words[:].bitcast(I32), in_=Wq_words[0].bitcast(I32))
@@ -67,12 +70,12 @@ def tile_ufoattention_pb_t_kernel(tc, queries, Wq_words, Wq_scales, bq, gamma, o
                 out=w_scales[32 * quad : 32 * quad + 4, :].bitcast(I32),
                 in_=Wq_scales[0, 4 * quad : 4 * quad + 4, :].bitcast(I32),
             )
-        for c in range(1, AHEAD):
+        for c in range(2, AHEAD):
             load(c)
 
         one = consts.tile([P, 1], F32)
         nc.vector.memset(one[:], 1.0)
-        nc.scalar.activation(out=one[:], in_=one[:], func=SQRT)
+        nc.scalar.activation(out=one[:], in_=one[:], func=RSQRT)
 
         ident = consts.tile([P, P], F32)
         make_identity(nc, ident[:])
@@ -109,11 +112,11 @@ def tile_ufoattention_pb_t_kernel(tc, queries, Wq_words, Wq_scales, bq, gamma, o
                         nc.tensor.transpose(
                             xt[:, i, u, :], x_words[:, j * WORDS + u : (j + 1) * WORDS : 2], ident[:]
                         )
-                grouped_part = grouped_words[:, bank * PER_BANK : (bank + 1) * PER_BANK, :, :]
-                if bank % 2 == 0:
-                    nc.scalar.copy(out=grouped_part, in_=xt[:].rearrange("p i u c -> p i c u"))
-                else:
-                    nc.vector.tensor_copy(out=grouped_part, in_=xt[:].rearrange("p i u c -> p i c u"))
+                copy = nc.vector.tensor_copy if bank == BANKS - 1 else nc.scalar.copy
+                copy(
+                    out=grouped_words[:, bank * PER_BANK : (bank + 1) * PER_BANK, :, :],
+                    in_=xt[:].rearrange("p i u c -> p i c u"),
+                )
             grouped_tiles[c] = grouped
 
         def quantise(c):
@@ -153,7 +156,7 @@ def tile_ufoattention_pb_t_kernel(tc, queries, Wq_words, Wq_scales, bq, gamma, o
                 )
             q_tiles[c] = q_sb
 
-        def norms(c):
+        def sum_squares(c):
             q_sb = q_tiles[c]
             squares = squares_pool.tile([P, HEADS, SUB, HEAD_DIM], F32)
             sums = stats_pool.tile([P, HEADS, SUB], F32)
@@ -162,32 +165,32 @@ def tile_ufoattention_pb_t_kernel(tc, queries, Wq_words, Wq_scales, bq, gamma, o
                     nc.scalar.activation(
                         out=squares[:, h, j, :], in_=q_sb[:, h, j, :], func=SQUARE, accum_out=sums[:, h, j : j + 1]
                     )
-            norm = stats_pool.tile([P, HEADS, SUB], F32)
-            nc.scalar.activation(out=norm[:], in_=sums[:], func=SQRT)
-            norm_tiles[c] = norm
+            sum_tiles[c] = sums
+
+        def inverse_norms(c):
+            inverse = stats_pool.tile([P, HEADS, SUB], F32)
+            nc.scalar.activation(out=inverse[:], in_=sum_tiles[c][:], func=RSQRT)
+            inverse_tiles[c] = inverse
 
         def scale_and_store(c):
             batch, part = divmod(c, CHUNKS_PER_BATCH)
-            q_sb, norm = q_tiles[c], norm_tiles[c]
-            factor = stats_pool.tile([P, HEADS, SUB], F32)
-            nc.vector.reciprocal(out=factor[:], in_=norm[:])
-            nc.vector.tensor_tensor(
-                out=factor[:], in0=factor[:], in1=gain[:].unsqueeze(2).to_broadcast([P, HEADS, SUB]), op=MULT
-            )
+            q_sb, inverse = q_tiles[c], inverse_tiles[c]
             for h in range(HEADS):
-                engine = nc.gpsimd if h < GPSIMD_HEADS else nc.vector
-                engine.tensor_tensor(
-                    out=q_sb[:, h, :, :],
-                    in0=q_sb[:, h, :, :],
-                    in1=factor[:, h, :].unsqueeze(2).to_broadcast([P, SUB, HEAD_DIM]),
-                    op=MULT,
+                for j in range(SUB):
+                    nc.vector.tensor_scalar(
+                        out=q_sb[:, h, j, :],
+                        in0=q_sb[:, h, j, :],
+                        scalar1=inverse[:, h, j : j + 1],
+                        scalar2=gain[:, h : h + 1],
+                        op0=MULT,
+                        op1=MULT,
+                    )
+                rows = out[batch, h, part * CHUNK : (part + 1) * CHUNK, :]
+                nc.sync.dma_start(
+                    out=rows.rearrange("(p j) d -> p (j d)", j=SUB), in_=q_sb[:, h, :, :].rearrange("p j d -> p (j d)")
                 )
-            rows = out[batch, :, part * CHUNK : (part + 1) * CHUNK, :]
-            nc.sync.dma_start(
-                out=rows.rearrange("h (p j) d -> p h (j d)", j=SUB), in_=q_sb[:].rearrange("p h j d -> p h (j d)")
-            )
 
-        for s in range(N_CHUNKS + 3):
+        for s in range(N_CHUNKS + 4):
             if s + AHEAD < N_CHUNKS:
                 load(s + AHEAD)
             if 0 <= s - 1 < N_CHUNKS:
@@ -196,9 +199,11 @@ def tile_ufoattention_pb_t_kernel(tc, queries, Wq_words, Wq_scales, bq, gamma, o
                 transpose_and_group(s)
             if 0 <= s - 1 < N_CHUNKS:
                 project(s - 1)
-            if 0 <= s - 3:
-                scale_and_store(s - 3)
+            if 0 <= s - 3 < N_CHUNKS:
+                inverse_norms(s - 3)
+            if 0 <= s - 4 < N_CHUNKS:
+                scale_and_store(s - 4)
             if 0 <= s - 1 < N_CHUNKS:
                 add_bias(s - 1)
             if 0 <= s - 2 < N_CHUNKS:
-                norms(s - 2)
+                sum_squares(s - 2)

@@ -27,7 +27,7 @@ N_CHUNKS = BATCH * CHUNKS_PER_BATCH
 PER_BANK = 2
 BANKS = SUB // PER_BANK
 AHEAD = 3
-FIRST_LOAD_PIECES = 2
+FIRST_LOAD_PIECES = BANKS
 
 FLOPS = 2 * BATCH * TOKENS * K * FEATURES
 
@@ -40,7 +40,7 @@ def tile_ufoattention_pb_t_kernel(tc, queries, Wq_words, Wq_scales, bq, gamma, o
         x_pool = ctx.enter_context(tc.tile_pool(name="x", bufs=AHEAD + 1))
         grouped_pool = ctx.enter_context(tc.tile_pool(name="grouped", bufs=2))
         mx_pool = ctx.enter_context(tc.tile_pool(name="mx", bufs=2))
-        q_pool = ctx.enter_context(tc.tile_pool(name="q", bufs=6))
+        q_pool = ctx.enter_context(tc.tile_pool(name="q", bufs=5))
         squares_pool = ctx.enter_context(tc.tile_pool(name="squares", bufs=2))
         stats_pool = ctx.enter_context(tc.tile_pool(name="stats", bufs=3))
         xt_pool = ctx.enter_context(tc.psum_pool(name="xt", bufs=BANKS))
@@ -70,7 +70,7 @@ def tile_ufoattention_pb_t_kernel(tc, queries, Wq_words, Wq_scales, bq, gamma, o
                 out=w_scales[32 * quad : 32 * quad + 4, :].bitcast(I32),
                 in_=Wq_scales[0, 4 * quad : 4 * quad + 4, :].bitcast(I32),
             )
-        for c in range(2, AHEAD):
+        for c in range(2, AHEAD + 1):
             load(c)
 
         one = consts.tile([P, 1], F32)
@@ -89,16 +89,6 @@ def tile_ufoattention_pb_t_kernel(tc, queries, Wq_words, Wq_scales, bq, gamma, o
         )
         ones = consts.tile([P, P], BF16)
         nc.vector.memset(ones[:], 1.0)
-        spread = y_pool.tile([P, PER_BANK, FEATURES], F32, tag="y_ps")
-        nc.tensor.matmul(
-            out=spread[:].rearrange("p a n -> p (a n)"), lhsT=ones[:], rhs=vectors[:], start=True, stop=True
-        )
-        bias = consts.tile([P, PER_BANK, FEATURES], F32)
-        nc.vector.tensor_copy(
-            out=bias[:], in_=spread[:, 0:1, :].to_broadcast([P, PER_BANK, FEATURES])
-        )
-        gain = consts.tile([P, HEADS], F32)
-        nc.vector.tensor_copy(out=gain[:], in_=spread[:, 1, 0:HEADS])
 
         def transpose_and_group(c):
             x_words = x_tiles[c][:].bitcast(F32)
@@ -160,8 +150,8 @@ def tile_ufoattention_pb_t_kernel(tc, queries, Wq_words, Wq_scales, bq, gamma, o
             q_sb = q_tiles[c]
             squares = squares_pool.tile([P, HEADS, SUB, HEAD_DIM], F32)
             sums = stats_pool.tile([P, HEADS, SUB], F32)
-            for h in range(HEADS):
-                for j in range(SUB):
+            for j in range(SUB):
+                for h in range(HEADS):
                     nc.scalar.activation(
                         out=squares[:, h, j, :], in_=q_sb[:, h, j, :], func=SQUARE, accum_out=sums[:, h, j : j + 1]
                     )
@@ -190,7 +180,20 @@ def tile_ufoattention_pb_t_kernel(tc, queries, Wq_words, Wq_scales, bq, gamma, o
                     out=rows.rearrange("(p j) d -> p (j d)", j=SUB), in_=q_sb[:, h, :, :].rearrange("p j d -> p (j d)")
                 )
 
-        for s in range(N_CHUNKS + 4):
+        transpose_and_group(0)
+
+        spread = y_pool.tile([P, PER_BANK, FEATURES], F32, tag="y_ps")
+        nc.tensor.matmul(
+            out=spread[:].rearrange("p a n -> p (a n)"), lhsT=ones[:], rhs=vectors[:], start=True, stop=True
+        )
+        bias = consts.tile([P, PER_BANK, FEATURES], F32)
+        nc.vector.tensor_copy(
+            out=bias[:], in_=spread[:, 0:1, :].to_broadcast([P, PER_BANK, FEATURES])
+        )
+        gain = consts.tile([P, HEADS], F32)
+        nc.vector.tensor_copy(out=gain[:], in_=spread[:, 1, 0:HEADS])
+
+        for s in range(1, N_CHUNKS + 3):
             if s + AHEAD < N_CHUNKS:
                 load(s + AHEAD)
             if 0 <= s - 1 < N_CHUNKS:
@@ -199,11 +202,11 @@ def tile_ufoattention_pb_t_kernel(tc, queries, Wq_words, Wq_scales, bq, gamma, o
                 transpose_and_group(s)
             if 0 <= s - 1 < N_CHUNKS:
                 project(s - 1)
-            if 0 <= s - 3 < N_CHUNKS:
-                inverse_norms(s - 3)
-            if 0 <= s - 4 < N_CHUNKS:
-                scale_and_store(s - 4)
             if 0 <= s - 1 < N_CHUNKS:
                 add_bias(s - 1)
             if 0 <= s - 2 < N_CHUNKS:
-                sum_squares(s - 2)
+                inverse_norms(s - 2)
+            if 0 <= s - 1 < N_CHUNKS:
+                sum_squares(s - 1)
+            if 0 <= s - 3 < N_CHUNKS:
+                scale_and_store(s - 3)

@@ -40,7 +40,7 @@ def tile_ufoattention_pb_t_kernel(tc, queries, Wq_words, Wq_scales, bq, gamma, o
         x_pool = ctx.enter_context(tc.tile_pool(name="x", bufs=AHEAD + 1))
         grouped_pool = ctx.enter_context(tc.tile_pool(name="grouped", bufs=2))
         mx_pool = ctx.enter_context(tc.tile_pool(name="mx", bufs=2))
-        q_pool = ctx.enter_context(tc.tile_pool(name="q", bufs=5))
+        q_pool = ctx.enter_context(tc.tile_pool(name="q", bufs=6))
         squares_pool = ctx.enter_context(tc.tile_pool(name="squares", bufs=2))
         stats_pool = ctx.enter_context(tc.tile_pool(name="stats", bufs=3))
         xt_pool = ctx.enter_context(tc.psum_pool(name="xt", bufs=BANKS))
@@ -150,8 +150,8 @@ def tile_ufoattention_pb_t_kernel(tc, queries, Wq_words, Wq_scales, bq, gamma, o
             q_sb = q_tiles[c]
             squares = squares_pool.tile([P, HEADS, SUB, HEAD_DIM], F32)
             sums = stats_pool.tile([P, HEADS, SUB], F32)
-            for j in range(SUB):
-                for h in range(HEADS):
+            for h in range(HEADS):
+                for j in range(SUB):
                     nc.scalar.activation(
                         out=squares[:, h, j, :], in_=q_sb[:, h, j, :], func=SQUARE, accum_out=sums[:, h, j : j + 1]
                     )
@@ -193,7 +193,7 @@ def tile_ufoattention_pb_t_kernel(tc, queries, Wq_words, Wq_scales, bq, gamma, o
         gain = consts.tile([P, HEADS], F32)
         nc.vector.tensor_copy(out=gain[:], in_=spread[:, 1, 0:HEADS])
 
-        for s in range(1, N_CHUNKS + 3):
+        for s in range(1, N_CHUNKS + 4):
             if s + AHEAD < N_CHUNKS:
                 load(s + AHEAD)
             if 0 <= s - 1 < N_CHUNKS:
@@ -202,11 +202,11 @@ def tile_ufoattention_pb_t_kernel(tc, queries, Wq_words, Wq_scales, bq, gamma, o
                 transpose_and_group(s)
             if 0 <= s - 1 < N_CHUNKS:
                 project(s - 1)
+            if 0 <= s - 3 < N_CHUNKS:
+                inverse_norms(s - 3)
+            if 0 <= s - 4 < N_CHUNKS:
+                scale_and_store(s - 4)
             if 0 <= s - 1 < N_CHUNKS:
                 add_bias(s - 1)
             if 0 <= s - 2 < N_CHUNKS:
-                inverse_norms(s - 2)
-            if 0 <= s - 1 < N_CHUNKS:
-                sum_squares(s - 1)
-            if 0 <= s - 3 < N_CHUNKS:
-                scale_and_store(s - 3)
+                sum_squares(s - 2)

@@ -14,6 +14,7 @@ ADD = mybir.AluOpType.add
 MULT = mybir.AluOpType.mult
 SQUARE = mybir.ActivationFunctionType.Square
 RSQRT = mybir.ActivationFunctionType.Abs_reciprocal_sqrt
+COPY = mybir.ActivationFunctionType.Copy
 
 P = 128
 BATCH, TOKENS, K = 4, 4096, 512
@@ -28,6 +29,8 @@ PER_BANK = 2
 BANKS = SUB // PER_BANK
 AHEAD = 3
 FIRST_LOAD_PIECES = BANKS
+POOL_HEADS = 3
+SCALAR_COPY_BANKS = 1
 
 FLOPS = 2 * BATCH * TOKENS * K * FEATURES
 
@@ -47,7 +50,7 @@ def tile_ufoattention_pb_t_kernel(tc, queries, Wq_words, Wq_scales, bq, gamma, o
         y_pool = ctx.enter_context(tc.psum_pool(name="y", bufs=BANKS))
 
         x_tiles, grouped_tiles, code_tiles, plane_tiles = {}, {}, {}, {}
-        y_tiles, q_tiles, sum_tiles, inverse_tiles = {}, {}, {}, {}
+        y_tiles, q_tiles, sum_tiles, inverse_tiles, factor_tiles = {}, {}, {}, {}, {}
 
         def load(c, pieces=1):
             batch, part = divmod(c, CHUNKS_PER_BATCH)
@@ -102,7 +105,7 @@ def tile_ufoattention_pb_t_kernel(tc, queries, Wq_words, Wq_scales, bq, gamma, o
                         nc.tensor.transpose(
                             xt[:, i, u, :], x_words[:, j * WORDS + u : (j + 1) * WORDS : 2], ident[:]
                         )
-                copy = nc.vector.tensor_copy if bank == BANKS - 1 else nc.scalar.copy
+                copy = nc.scalar.copy if bank < SCALAR_COPY_BANKS else nc.vector.tensor_copy
                 copy(
                     out=grouped_words[:, bank * PER_BANK : (bank + 1) * PER_BANK, :, :],
                     in_=xt[:].rearrange("p i u c -> p i c u"),
@@ -162,23 +165,40 @@ def tile_ufoattention_pb_t_kernel(tc, queries, Wq_words, Wq_scales, bq, gamma, o
             nc.scalar.activation(out=inverse[:], in_=sum_tiles[c][:], func=RSQRT)
             inverse_tiles[c] = inverse
 
-        def scale_and_store(c):
+        def factors(c):
+            factor = stats_pool.tile([P, HEADS, SUB, 1], F32)
+            nc.vector.tensor_tensor(
+                out=factor[:].rearrange("p h j o -> p h (j o)"),
+                in0=inverse_tiles[c][:],
+                in1=gain[:].to_broadcast([P, HEADS, SUB]),
+                op=MULT,
+            )
+            factor_tiles[c] = factor
+
+        def store(c, h):
             batch, part = divmod(c, CHUNKS_PER_BATCH)
-            q_sb, inverse = q_tiles[c], inverse_tiles[c]
-            for h in range(HEADS):
+            rows = out[batch, h, part * CHUNK : (part + 1) * CHUNK, :]
+            nc.sync.dma_start(
+                out=rows.rearrange("(p j) d -> p (j d)", j=SUB), in_=q_tiles[c][:, h, :, :].rearrange("p j d -> p (j d)")
+            )
+
+        def scale_on_gpsimd(c):
+            q_sb, factor = q_tiles[c], factor_tiles[c]
+            nc.gpsimd.tensor_tensor(
+                out=q_sb[:, 0:POOL_HEADS, :, :],
+                in0=q_sb[:, 0:POOL_HEADS, :, :],
+                in1=factor[:, 0:POOL_HEADS, :, :].to_broadcast([P, POOL_HEADS, SUB, HEAD_DIM]),
+                op=MULT,
+            )
+            for h in range(POOL_HEADS):
+                store(c, h)
+
+        def scale_on_scalar(c):
+            q_sb, factor = q_tiles[c], factor_tiles[c]
+            for h in range(POOL_HEADS, HEADS):
                 for j in range(SUB):
-                    nc.vector.tensor_scalar(
-                        out=q_sb[:, h, j, :],
-                        in0=q_sb[:, h, j, :],
-                        scalar1=inverse[:, h, j : j + 1],
-                        scalar2=gain[:, h : h + 1],
-                        op0=MULT,
-                        op1=MULT,
-                    )
-                rows = out[batch, h, part * CHUNK : (part + 1) * CHUNK, :]
-                nc.sync.dma_start(
-                    out=rows.rearrange("(p j) d -> p (j d)", j=SUB), in_=q_sb[:, h, :, :].rearrange("p j d -> p (j d)")
-                )
+                    nc.scalar.activation(out=q_sb[:, h, j, :], in_=q_sb[:, h, j, :], func=COPY, scale=factor[:, h, j, :])
+                store(c, h)
 
         transpose_and_group(0)
 
@@ -190,23 +210,25 @@ def tile_ufoattention_pb_t_kernel(tc, queries, Wq_words, Wq_scales, bq, gamma, o
         nc.vector.tensor_copy(
             out=bias[:], in_=spread[:, 0:1, :].to_broadcast([P, PER_BANK, FEATURES])
         )
-        gain = consts.tile([P, HEADS], F32)
-        nc.vector.tensor_copy(out=gain[:], in_=spread[:, 1, 0:HEADS])
+        gain = consts.tile([P, HEADS, 1], F32)
+        nc.vector.tensor_copy(out=gain[:].rearrange("p h o -> p (h o)"), in_=spread[:, 1, 0:HEADS])
 
-        for s in range(1, N_CHUNKS + 4):
+        for s in range(1, N_CHUNKS + 3):
             if s + AHEAD < N_CHUNKS:
                 load(s + AHEAD)
+            if 0 <= s - 3 < N_CHUNKS:
+                inverse_norms(s - 3)
             if 0 <= s - 1 < N_CHUNKS:
                 quantise(s - 1)
+            if 0 <= s - 3 < N_CHUNKS:
+                factors(s - 3)
+                scale_on_gpsimd(s - 3)
             if s < N_CHUNKS:
                 transpose_and_group(s)
             if 0 <= s - 1 < N_CHUNKS:
                 project(s - 1)
-            if 0 <= s - 3 < N_CHUNKS:
-                inverse_norms(s - 3)
-            if 0 <= s - 4 < N_CHUNKS:
-                scale_and_store(s - 4)
-            if 0 <= s - 1 < N_CHUNKS:
                 add_bias(s - 1)
             if 0 <= s - 2 < N_CHUNKS:
                 sum_squares(s - 2)
+            if 0 <= s - 3 < N_CHUNKS:
+                scale_on_scalar(s - 3)

@@ -22,28 +22,46 @@ HEADS, HEAD_DIM = 4, 64
 FEATURES = HEADS * HEAD_DIM
 WORDS = K // 2
 SUB = 8
-CHUNK = P * SUB
-CHUNKS_PER_BATCH = TOKENS // CHUNK
-N_CHUNKS = BATCH * CHUNKS_PER_BATCH
 PER_BANK = 2
 BANKS = SUB // PER_BANK
 AHEAD = 3
-FIRST_LOAD_PIECES = BANKS
+HEAD_SUBS = [2, 2, 4]
+TAIL_SUBS = []
+HEAD_CHUNKS = 5
+TAIL_CHUNKS = 3
 POOL_HEADS = 3
 SCALAR_COPY_BANKS = 1
 
 FLOPS = 2 * BATCH * TOKENS * K * FEATURES
 
 
+def chunk_list():
+    chunks = []
+    for batch in range(BATCH):
+        subs = [SUB] * (TOKENS // (P * SUB))
+        if batch == 0:
+            subs = HEAD_SUBS + subs[sum(HEAD_SUBS) // SUB :]
+        if batch == BATCH - 1:
+            subs = subs[: len(subs) - sum(TAIL_SUBS) // SUB] + TAIL_SUBS
+        first = 0
+        for sub in subs:
+            chunks.append((batch, first, sub))
+            first += P * sub
+        assert first == TOKENS
+    return chunks
+
+
 def tile_ufoattention_pb_t_kernel(tc, queries, Wq_words, Wq_scales, bq, gamma, out):
     nc = tc.nc
+    chunks = chunk_list()
+    n_chunks = len(chunks)
     with ExitStack() as ctx:
         ctx.enter_context(tc.manual_schedule())
         consts = ctx.enter_context(tc.tile_pool(name="consts", bufs=1))
         x_pool = ctx.enter_context(tc.tile_pool(name="x", bufs=AHEAD + 1))
         grouped_pool = ctx.enter_context(tc.tile_pool(name="grouped", bufs=2))
         mx_pool = ctx.enter_context(tc.tile_pool(name="mx", bufs=2))
-        q_pool = ctx.enter_context(tc.tile_pool(name="q", bufs=6))
+        q_pool = ctx.enter_context(tc.tile_pool(name="q", bufs=8))
         squares_pool = ctx.enter_context(tc.tile_pool(name="squares", bufs=2))
         stats_pool = ctx.enter_context(tc.tile_pool(name="stats", bufs=3))
         xt_pool = ctx.enter_context(tc.psum_pool(name="xt", bufs=BANKS))
@@ -52,16 +70,15 @@ def tile_ufoattention_pb_t_kernel(tc, queries, Wq_words, Wq_scales, bq, gamma, o
         x_tiles, grouped_tiles, code_tiles, plane_tiles = {}, {}, {}, {}
         y_tiles, q_tiles, sum_tiles, inverse_tiles, factor_tiles = {}, {}, {}, {}, {}
 
-        def load(c, pieces=1):
-            batch, part = divmod(c, CHUNKS_PER_BATCH)
-            x_sb = x_pool.tile([P, SUB * K], BF16)
-            rows = queries[batch, part * CHUNK : (part + 1) * CHUNK, :].rearrange("(p j) k -> p (j k)", j=SUB)
-            width = SUB * K // pieces
-            for i in range(pieces):
-                nc.sync.dma_start(out=x_sb[:, i * width : (i + 1) * width], in_=rows[:, i * width : (i + 1) * width])
+        def load(c):
+            batch, first, sub = chunks[c]
+            x_sb = x_pool.tile([P, sub * K], BF16)
+            nc.sync.dma_start(
+                out=x_sb[:], in_=queries[batch, first : first + P * sub, :].rearrange("(p j) k -> p (j k)", j=sub)
+            )
             x_tiles[c] = x_sb
 
-        load(0, pieces=FIRST_LOAD_PIECES)
+        load(0)
         load(1)
 
         w_words = consts.tile([P, 2 * FEATURES], U8, align_bytes=64)
@@ -94,10 +111,11 @@ def tile_ufoattention_pb_t_kernel(tc, queries, Wq_words, Wq_scales, bq, gamma, o
         nc.vector.memset(ones[:], 1.0)
 
         def transpose_and_group(c):
+            sub = chunks[c][2]
             x_words = x_tiles[c][:].bitcast(F32)
-            grouped = grouped_pool.tile([P, SUB * P * 4], BF16, align_bytes=64)
-            grouped_words = grouped[:].bitcast(F32).rearrange("p (j c u) -> p j c u", j=SUB, u=2)
-            for bank in range(BANKS):
+            grouped = grouped_pool.tile([P, sub * P * 4], BF16, align_bytes=64)
+            grouped_words = grouped[:].bitcast(F32).rearrange("p (j c u) -> p j c u", j=sub, u=2)
+            for bank in range(sub // PER_BANK):
                 xt = xt_pool.tile([P, PER_BANK, 2, P], F32)
                 for i in range(PER_BANK):
                     j = bank * PER_BANK + i
@@ -105,7 +123,8 @@ def tile_ufoattention_pb_t_kernel(tc, queries, Wq_words, Wq_scales, bq, gamma, o
                         nc.tensor.transpose(
                             xt[:, i, u, :], x_words[:, j * WORDS + u : (j + 1) * WORDS : 2], ident[:]
                         )
-                copy = nc.scalar.copy if bank < SCALAR_COPY_BANKS else nc.vector.tensor_copy
+                on_scalar = c < HEAD_CHUNKS or bank < SCALAR_COPY_BANKS
+                copy = nc.scalar.copy if on_scalar else nc.vector.tensor_copy
                 copy(
                     out=grouped_words[:, bank * PER_BANK : (bank + 1) * PER_BANK, :, :],
                     in_=xt[:].rearrange("p i u c -> p i c u"),
@@ -113,8 +132,9 @@ def tile_ufoattention_pb_t_kernel(tc, queries, Wq_words, Wq_scales, bq, gamma, o
             grouped_tiles[c] = grouped
 
         def quantise(c):
-            codes = mx_pool.tile([P, CHUNK], U32, align_bytes=64)
-            planes = mx_pool.tile([P, CHUNK], U8, align_bytes=64)
+            sub = chunks[c][2]
+            codes = mx_pool.tile([P, sub * P], U32, align_bytes=64)
+            planes = mx_pool.tile([P, sub * P], U8, align_bytes=64)
             nc.vector.quantize_mx(
                 out=codes[:].bitcast(FP8X4), scales=planes[:], in_=grouped_tiles[c][:]
             )
@@ -123,7 +143,7 @@ def tile_ufoattention_pb_t_kernel(tc, queries, Wq_words, Wq_scales, bq, gamma, o
         def project(c):
             codes, planes = code_tiles[c], plane_tiles[c]
             y_tiles[c] = []
-            for bank in range(BANKS):
+            for bank in range(chunks[c][2] // PER_BANK):
                 y_ps = y_pool.tile([P, PER_BANK, FEATURES], F32)
                 for i in range(PER_BANK):
                     cols = slice((bank * PER_BANK + i) * P, (bank * PER_BANK + i + 1) * P)
@@ -139,7 +159,7 @@ def tile_ufoattention_pb_t_kernel(tc, queries, Wq_words, Wq_scales, bq, gamma, o
                 y_tiles[c].append(y_ps)
 
         def add_bias(c):
-            q_sb = q_pool.tile([P, HEADS, SUB, HEAD_DIM], F32)
+            q_sb = q_pool.tile([P, HEADS, chunks[c][2], HEAD_DIM], F32)
             for bank, y_ps in enumerate(y_tiles[c]):
                 nc.vector.tensor_tensor(
                     out=q_sb[:, :, bank * PER_BANK : (bank + 1) * PER_BANK, :].rearrange("p h i d -> p i h d"),
@@ -150,44 +170,44 @@ def tile_ufoattention_pb_t_kernel(tc, queries, Wq_words, Wq_scales, bq, gamma, o
             q_tiles[c] = q_sb
 
         def sum_squares(c):
+            sub = chunks[c][2]
             q_sb = q_tiles[c]
-            squares = squares_pool.tile([P, HEADS, SUB, HEAD_DIM], F32)
-            sums = stats_pool.tile([P, HEADS, SUB], F32)
-            for h in range(HEADS):
-                for j in range(SUB):
+            squares = squares_pool.tile([P, HEADS, sub, HEAD_DIM], F32)
+            sums = stats_pool.tile([P, HEADS, sub], F32)
+            for j in range(sub):
+                for h in range(HEADS):
                     nc.scalar.activation(
                         out=squares[:, h, j, :], in_=q_sb[:, h, j, :], func=SQUARE, accum_out=sums[:, h, j : j + 1]
                     )
             sum_tiles[c] = sums
 
         def inverse_norms(c):
-            inverse = stats_pool.tile([P, HEADS, SUB], F32)
+            inverse = stats_pool.tile([P, HEADS, chunks[c][2]], F32)
             nc.scalar.activation(out=inverse[:], in_=sum_tiles[c][:], func=RSQRT)
             inverse_tiles[c] = inverse
 
-        def factors(c):
-            factor = stats_pool.tile([P, HEADS, SUB, 1], F32)
+        def store(c, h):
+            batch, first, sub = chunks[c]
+            nc.sync.dma_start(
+                out=out[batch, h, first : first + P * sub, :].rearrange("(p j) d -> p (j d)", j=sub),
+                in_=q_tiles[c][:, h, :, :].rearrange("p j d -> p (j d)"),
+            )
+
+        def factors_and_gpsimd(c):
+            sub = chunks[c][2]
+            q_sb = q_tiles[c]
+            factor = stats_pool.tile([P, HEADS, sub, 1], F32)
             nc.vector.tensor_tensor(
                 out=factor[:].rearrange("p h j o -> p h (j o)"),
                 in0=inverse_tiles[c][:],
-                in1=gain[:].to_broadcast([P, HEADS, SUB]),
+                in1=gain[:].to_broadcast([P, HEADS, sub]),
                 op=MULT,
             )
             factor_tiles[c] = factor
-
-        def store(c, h):
-            batch, part = divmod(c, CHUNKS_PER_BATCH)
-            rows = out[batch, h, part * CHUNK : (part + 1) * CHUNK, :]
-            nc.sync.dma_start(
-                out=rows.rearrange("(p j) d -> p (j d)", j=SUB), in_=q_tiles[c][:, h, :, :].rearrange("p j d -> p (j d)")
-            )
-
-        def scale_on_gpsimd(c):
-            q_sb, factor = q_tiles[c], factor_tiles[c]
             nc.gpsimd.tensor_tensor(
                 out=q_sb[:, 0:POOL_HEADS, :, :],
                 in0=q_sb[:, 0:POOL_HEADS, :, :],
-                in1=factor[:, 0:POOL_HEADS, :, :].to_broadcast([P, POOL_HEADS, SUB, HEAD_DIM]),
+                in1=factor[:, 0:POOL_HEADS, :, :].to_broadcast([P, POOL_HEADS, sub, HEAD_DIM]),
                 op=MULT,
             )
             for h in range(POOL_HEADS):
@@ -196,8 +216,22 @@ def tile_ufoattention_pb_t_kernel(tc, queries, Wq_words, Wq_scales, bq, gamma, o
         def scale_on_scalar(c):
             q_sb, factor = q_tiles[c], factor_tiles[c]
             for h in range(POOL_HEADS, HEADS):
-                for j in range(SUB):
+                for j in range(chunks[c][2]):
                     nc.scalar.activation(out=q_sb[:, h, j, :], in_=q_sb[:, h, j, :], func=COPY, scale=factor[:, h, j, :])
+                store(c, h)
+
+        def scale_on_vector(c):
+            q_sb, inverse = q_tiles[c], inverse_tiles[c]
+            for h in range(HEADS):
+                for j in range(chunks[c][2]):
+                    nc.vector.tensor_scalar(
+                        out=q_sb[:, h, j, :],
+                        in0=q_sb[:, h, j, :],
+                        scalar1=inverse[:, h, j : j + 1],
+                        scalar2=gain[:, h, :],
+                        op0=MULT,
+                        op1=MULT,
+                    )
                 store(c, h)
 
         transpose_and_group(0)
@@ -213,22 +247,26 @@ def tile_ufoattention_pb_t_kernel(tc, queries, Wq_words, Wq_scales, bq, gamma, o
         gain = consts.tile([P, HEADS, 1], F32)
         nc.vector.tensor_copy(out=gain[:].rearrange("p h o -> p (h o)"), in_=spread[:, 1, 0:HEADS])
 
-        for s in range(1, N_CHUNKS + 3):
-            if s + AHEAD < N_CHUNKS:
+        for s in range(1, n_chunks + 3):
+            scaled = s - 3
+            by_vector = scaled >= n_chunks - TAIL_CHUNKS
+            if s + AHEAD < n_chunks:
                 load(s + AHEAD)
-            if 0 <= s - 3 < N_CHUNKS:
-                inverse_norms(s - 3)
-            if 0 <= s - 1 < N_CHUNKS:
+            if 0 <= scaled:
+                inverse_norms(scaled)
+            if s - 1 < n_chunks:
                 quantise(s - 1)
-            if 0 <= s - 3 < N_CHUNKS:
-                factors(s - 3)
-                scale_on_gpsimd(s - 3)
-            if s < N_CHUNKS:
+            if 0 <= scaled and not by_vector:
+                factors_and_gpsimd(scaled)
+            if s < n_chunks:
                 transpose_and_group(s)
-            if 0 <= s - 1 < N_CHUNKS:
+            if 0 <= scaled:
+                if by_vector:
+                    scale_on_vector(scaled)
+                else:
+                    scale_on_scalar(scaled)
+            if s - 1 < n_chunks:
                 project(s - 1)
                 add_bias(s - 1)
-            if 0 <= s - 2 < N_CHUNKS:
+            if 0 <= s - 2 < n_chunks:
                 sum_squares(s - 2)
-            if 0 <= s - 3 < N_CHUNKS:
-                scale_on_scalar(s - 3)

@@ -247,26 +247,27 @@ def tile_ufoattention_pb_t_kernel(tc, queries, Wq_words, Wq_scales, bq, gamma, o
         gain = consts.tile([P, HEADS, 1], F32)
         nc.vector.tensor_copy(out=gain[:].rearrange("p h o -> p (h o)"), in_=spread[:, 1, 0:HEADS])
 
-        for s in range(1, n_chunks + 3):
-            scaled = s - 3
-            by_vector = scaled >= n_chunks - TAIL_CHUNKS
+        for s in range(1, n_chunks + 4):
+            late = s - 4
+            soon = s - 3
+            late_now = 0 <= late < n_chunks - TAIL_CHUNKS
+            soon_now = n_chunks - TAIL_CHUNKS <= soon < n_chunks
             if s + AHEAD < n_chunks:
                 load(s + AHEAD)
-            if 0 <= scaled:
-                inverse_norms(scaled)
             if s - 1 < n_chunks:
                 quantise(s - 1)
-            if 0 <= scaled and not by_vector:
-                factors_and_gpsimd(scaled)
+            if late_now:
+                factors_and_gpsimd(late)
             if s < n_chunks:
                 transpose_and_group(s)
-            if 0 <= scaled:
-                if by_vector:
-                    scale_on_vector(scaled)
-                else:
-                    scale_on_scalar(scaled)
+            if 0 <= s - 3 < n_chunks:
+                inverse_norms(s - 3)
+            if soon_now:
+                scale_on_vector(soon)
             if s - 1 < n_chunks:
                 project(s - 1)
                 add_bias(s - 1)
             if 0 <= s - 2 < n_chunks:
                 sum_squares(s - 2)
+            if late_now:
+                scale_on_scalar(late)

@@ -30,7 +30,7 @@ TAIL_SUBS = []
 HEAD_CHUNKS = 5
 TAIL_CHUNKS = 3
 POOL_HEADS = 3
-SCALAR_COPY_BANKS = 1
+SCALAR_COPY_BANKS = 2
 
 FLOPS = 2 * BATCH * TOKENS * K * FEATURES
 

@@ -12,9 +12,9 @@ FP8X4 = mybir.dt.float8_e4m3fn_x4
 FP4X4 = mybir.dt.float4_e2m1fn_x4
 ADD = mybir.AluOpType.add
 MULT = mybir.AluOpType.mult
+X_AXIS = mybir.AxisListType.X
 SQUARE = mybir.ActivationFunctionType.Square
 RSQRT = mybir.ActivationFunctionType.Abs_reciprocal_sqrt
-COPY = mybir.ActivationFunctionType.Copy
 
 P = 128
 BATCH, TOKENS, K = 4, 4096, 512
@@ -28,9 +28,10 @@ AHEAD = 3
 HEAD_SUBS = [2, 2, 4]
 TAIL_SUBS = []
 HEAD_CHUNKS = 5
-TAIL_CHUNKS = 3
+BY_HEAD_CHUNKS = 2
+LAST_VECTOR_HEADS = 1
 POOL_HEADS = 3
-SCALAR_COPY_BANKS = 2
+SCALAR_COPY_BANKS = (2, 3)
 
 FLOPS = 2 * BATCH * TOKENS * K * FEATURES
 
@@ -123,7 +124,7 @@ def tile_ufoattention_pb_t_kernel(tc, queries, Wq_words, Wq_scales, bq, gamma, o
                         nc.tensor.transpose(
                             xt[:, i, u, :], x_words[:, j * WORDS + u : (j + 1) * WORDS : 2], ident[:]
                         )
-                on_scalar = c < HEAD_CHUNKS or bank < SCALAR_COPY_BANKS
+                on_scalar = c < HEAD_CHUNKS or bank < SCALAR_COPY_BANKS[c % 2]
                 copy = nc.scalar.copy if on_scalar else nc.vector.tensor_copy
                 copy(
                     out=grouped_words[:, bank * PER_BANK : (bank + 1) * PER_BANK, :, :],
@@ -181,6 +182,39 @@ def tile_ufoattention_pb_t_kernel(tc, queries, Wq_words, Wq_scales, bq, gamma, o
                     )
             sum_tiles[c] = sums
 
+        def last_sums_on_vector(c):
+            sub = chunks[c][2]
+            q_part = q_tiles[c][:, HEADS - LAST_VECTOR_HEADS :, :, :]
+            sums = stats_pool.tile([P, HEADS, sub], F32)
+            products = squares_pool.tile([P, LAST_VECTOR_HEADS, sub, HEAD_DIM], F32)
+            nc.vector.tensor_tensor(out=products[:], in0=q_part, in1=q_part, op=MULT)
+            nc.vector.tensor_reduce(out=sums[:, HEADS - LAST_VECTOR_HEADS :, :], in_=products[:], axis=X_AXIS, op=ADD)
+            sum_tiles[c] = sums
+
+        def norms_and_scaling_by_head(c):
+            sub = chunks[c][2]
+            q_sb = q_tiles[c]
+            squares = squares_pool.tile([P, HEADS, sub, HEAD_DIM], F32)
+            inverse = stats_pool.tile([P, HEADS, sub], F32)
+            inverse_tiles[c] = inverse
+            by_scalar = HEADS
+            if c in sum_tiles:
+                sums = sum_tiles[c]
+                by_scalar = HEADS - LAST_VECTOR_HEADS
+                nc.scalar.activation(out=inverse[:, by_scalar:, :], in_=sums[:, by_scalar:, :], func=RSQRT)
+                scale_on_vector(c, range(by_scalar, HEADS))
+            else:
+                sums = stats_pool.tile([P, HEADS, sub], F32)
+            for h in range(by_scalar + 1):
+                if h < by_scalar:
+                    for j in range(sub):
+                        nc.scalar.activation(
+                            out=squares[:, h, j, :], in_=q_sb[:, h, j, :], func=SQUARE, accum_out=sums[:, h, j : j + 1]
+                        )
+                if h > 0:
+                    nc.scalar.activation(out=inverse[:, h - 1, :], in_=sums[:, h - 1, :], func=RSQRT)
+                    scale_on_vector(c, [h - 1])
+
         def inverse_norms(c):
             inverse = stats_pool.tile([P, HEADS, chunks[c][2]], F32)
             nc.scalar.activation(out=inverse[:], in_=sum_tiles[c][:], func=RSQRT)
@@ -213,16 +247,9 @@ def tile_ufoattention_pb_t_kernel(tc, queries, Wq_words, Wq_scales, bq, gamma, o
             for h in range(POOL_HEADS):
                 store(c, h)
 
-        def scale_on_scalar(c):
-            q_sb, factor = q_tiles[c], factor_tiles[c]
-            for h in range(POOL_HEADS, HEADS):
-                for j in range(chunks[c][2]):
-                    nc.scalar.activation(out=q_sb[:, h, j, :], in_=q_sb[:, h, j, :], func=COPY, scale=factor[:, h, j, :])
-                store(c, h)
-
-        def scale_on_vector(c):
+        def scale_on_vector(c, heads):
             q_sb, inverse = q_tiles[c], inverse_tiles[c]
-            for h in range(HEADS):
+            for h in heads:
                 for j in range(chunks[c][2]):
                     nc.vector.tensor_scalar(
                         out=q_sb[:, h, j, :],
@@ -247,27 +274,31 @@ def tile_ufoattention_pb_t_kernel(tc, queries, Wq_words, Wq_scales, bq, gamma, o
         gain = consts.tile([P, HEADS, 1], F32)
         nc.vector.tensor_copy(out=gain[:].rearrange("p h o -> p (h o)"), in_=spread[:, 1, 0:HEADS])
 
-        for s in range(1, n_chunks + 4):
+        last = n_chunks - 1
+        first_by_head = n_chunks - BY_HEAD_CHUNKS
+        first_without_gpsimd = first_by_head - 2
+        for s in range(1, n_chunks + 2):
             late = s - 4
-            soon = s - 3
-            late_now = 0 <= late < n_chunks - TAIL_CHUNKS
-            soon_now = n_chunks - TAIL_CHUNKS <= soon < n_chunks
             if s + AHEAD < n_chunks:
                 load(s + AHEAD)
             if s - 1 < n_chunks:
                 quantise(s - 1)
-            if late_now:
+            if 0 <= late < first_without_gpsimd:
+                scale_on_vector(late, range(POOL_HEADS, HEADS))
                 factors_and_gpsimd(late)
+            elif late == first_without_gpsimd:
+                scale_on_vector(late, range(HEADS))
             if s < n_chunks:
                 transpose_and_group(s)
-            if 0 <= s - 3 < n_chunks:
+            if 0 <= s - 3 < first_by_head:
                 inverse_norms(s - 3)
-            if soon_now:
-                scale_on_vector(soon)
             if s - 1 < n_chunks:
                 project(s - 1)
                 add_bias(s - 1)
-            if 0 <= s - 2 < n_chunks:
+            if s - 1 == last:
+                last_sums_on_vector(last)
+                scale_on_vector(first_by_head - 1, range(HEADS))
+            if 0 <= s - 2 < first_by_head:
                 sum_squares(s - 2)
-            if late_now:
-                scale_on_scalar(late)
+            elif first_by_head <= s - 2:
+                norms_and_scaling_by_head(s - 2)

@@ -15,6 +15,7 @@ MULT = mybir.AluOpType.mult
 X_AXIS = mybir.AxisListType.X
 SQUARE = mybir.ActivationFunctionType.Square
 RSQRT = mybir.ActivationFunctionType.Abs_reciprocal_sqrt
+COPY = mybir.ActivationFunctionType.Copy
 
 P = 128
 BATCH, TOKENS, K = 4, 4096, 512
@@ -31,7 +32,7 @@ HEAD_CHUNKS = 5
 BY_HEAD_CHUNKS = 2
 LAST_VECTOR_HEADS = 1
 POOL_HEADS = 3
-SCALAR_COPY_BANKS = (2, 3)
+SCALAR_COPY_BANKS = (1, 2)
 
 FLOPS = 2 * BATCH * TOKENS * K * FEATURES
 
@@ -247,6 +248,13 @@ def tile_ufoattention_pb_t_kernel(tc, queries, Wq_words, Wq_scales, bq, gamma, o
             for h in range(POOL_HEADS):
                 store(c, h)
 
+        def scale_on_scalar(c):
+            q_sb, factor = q_tiles[c], factor_tiles[c]
+            for h in range(POOL_HEADS, HEADS):
+                for j in range(chunks[c][2]):
+                    nc.scalar.activation(out=q_sb[:, h, j, :], in_=q_sb[:, h, j, :], func=COPY, scale=factor[:, h, j, :])
+                store(c, h)
+
         def scale_on_vector(c, heads):
             q_sb, inverse = q_tiles[c], inverse_tiles[c]
             for h in heads:
@@ -284,7 +292,6 @@ def tile_ufoattention_pb_t_kernel(tc, queries, Wq_words, Wq_scales, bq, gamma, o
             if s - 1 < n_chunks:
                 quantise(s - 1)
             if 0 <= late < first_without_gpsimd:
-                scale_on_vector(late, range(POOL_HEADS, HEADS))
                 factors_and_gpsimd(late)
             elif late == first_without_gpsimd:
                 scale_on_vector(late, range(HEADS))
@@ -300,5 +307,7 @@ def tile_ufoattention_pb_t_kernel(tc, queries, Wq_words, Wq_scales, bq, gamma, o
                 scale_on_vector(first_by_head - 1, range(HEADS))
             if 0 <= s - 2 < first_by_head:
                 sum_squares(s - 2)
+                if 0 <= late < first_without_gpsimd:
+                    scale_on_scalar(late)
             elif first_by_head <= s - 2:
                 norms_and_scaling_by_head(s - 2)

@@ -25,7 +25,7 @@ WORDS = K // 2
 SUB = 8
 PER_BANK = 2
 BANKS = SUB // PER_BANK
-AHEAD = 3
+AHEAD = 6
 HEAD_SUBS = [2, 2, 4]
 TAIL_SUBS = []
 HEAD_CHUNKS = 5
@@ -245,8 +245,11 @@ def tile_ufoattention_pb_t_kernel(tc, queries, Wq_words, Wq_scales, bq, gamma, o
                 in1=factor[:, 0:POOL_HEADS, :, :].to_broadcast([P, POOL_HEADS, sub, HEAD_DIM]),
                 op=MULT,
             )
-            for h in range(POOL_HEADS):
-                store(c, h)
+            batch, first, sub = chunks[c]
+            nc.sync.dma_start(
+                out=out[batch, 0:POOL_HEADS, first : first + P * sub, :].rearrange("h (p j) d -> p h (j d)", j=sub),
+                in_=q_sb[:, 0:POOL_HEADS, :, :].rearrange("p h j d -> p h (j d)"),
+            )
 
         def scale_on_scalar(c):
             q_sb, factor = q_tiles[c], factor_tiles[c]

@@ -80,6 +80,9 @@ def tile_ufoattention_pb_t_kernel(tc, queries, Wq_words, Wq_scales, bq, gamma, o
             )
             x_tiles[c] = x_sb
 
+        bias_row = consts.tile([P, FEATURES], BF16)
+        nc.vector.memset(bias_row[:], 0.0)
+        nc.scalar.dma_start(out=bias_row[0:1, :], in_=bq.rearrange("(a n) -> a n", a=1))
         load(0)
         load(1)
 
@@ -92,7 +95,11 @@ def tile_ufoattention_pb_t_kernel(tc, queries, Wq_words, Wq_scales, bq, gamma, o
                 out=w_scales[32 * quad : 32 * quad + 4, :].bitcast(I32),
                 in_=Wq_scales[0, 4 * quad : 4 * quad + 4, :].bitcast(I32),
             )
-        for c in range(2, AHEAD + 1):
+        load(2)
+        gain_row = consts.tile([P, HEADS], BF16)
+        nc.vector.memset(gain_row[:], 0.0)
+        nc.sync.dma_start(out=gain_row[0:1, :], in_=gamma.rearrange("a h b c -> a (h b c)"))
+        for c in range(3, AHEAD + 1):
             load(c)
 
         one = consts.tile([P, 1], F32)
@@ -102,13 +109,6 @@ def tile_ufoattention_pb_t_kernel(tc, queries, Wq_words, Wq_scales, bq, gamma, o
         ident = consts.tile([P, P], F32)
         make_identity(nc, ident[:])
 
-        vectors = consts.tile([P, PER_BANK * FEATURES], BF16)
-        nc.vector.memset(vectors[:], 0.0)
-        nc.scalar.dma_start(out=vectors[0:1, 0:FEATURES], in_=bq.rearrange("(a n) -> a n", a=1))
-        nc.scalar.dma_start(
-            out=vectors[0:1, FEATURES : FEATURES + HEADS],
-            in_=gamma.rearrange("a h b c -> a (h b c)"),
-        )
         ones = consts.tile([P, P], BF16)
         nc.vector.memset(ones[:], 1.0)
 
@@ -274,16 +274,18 @@ def tile_ufoattention_pb_t_kernel(tc, queries, Wq_words, Wq_scales, bq, gamma, o
 
         transpose_and_group(0)
 
-        spread = y_pool.tile([P, PER_BANK, FEATURES], F32, tag="y_ps")
-        nc.tensor.matmul(
-            out=spread[:].rearrange("p a n -> p (a n)"), lhsT=ones[:], rhs=vectors[:], start=True, stop=True
-        )
         bias = consts.tile([P, PER_BANK, FEATURES], F32)
-        nc.vector.tensor_copy(
-            out=bias[:], in_=spread[:, 0:1, :].to_broadcast([P, PER_BANK, FEATURES])
-        )
         gain = consts.tile([P, HEADS, 1], F32)
-        nc.vector.tensor_copy(out=gain[:].rearrange("p h o -> p (h o)"), in_=spread[:, 1, 0:HEADS])
+
+        def spread_bias():
+            spread = y_pool.tile([P, PER_BANK, FEATURES], F32, tag="y_ps")
+            nc.tensor.matmul(out=spread[:, 0, :], lhsT=ones[:], rhs=bias_row[:], start=True, stop=True)
+            nc.vector.tensor_copy(out=bias[:], in_=spread[:, 0:1, :].to_broadcast([P, PER_BANK, FEATURES]))
+
+        def spread_gain():
+            spread = y_pool.tile([P, PER_BANK, FEATURES], F32, tag="y_ps")
+            nc.tensor.matmul(out=spread[:, 0, 0:HEADS], lhsT=ones[:], rhs=gain_row[:], start=True, stop=True)
+            nc.vector.tensor_copy(out=gain[:].rearrange("p h o -> p (h o)"), in_=spread[:, 0, 0:HEADS])
 
         last = n_chunks - 1
         first_by_head = n_chunks - BY_HEAD_CHUNKS
@@ -302,6 +304,10 @@ def tile_ufoattention_pb_t_kernel(tc, queries, Wq_words, Wq_scales, bq, gamma, o
                 transpose_and_group(s)
             if 0 <= s - 3 < first_by_head:
                 inverse_norms(s - 3)
+            if s == 1:
+                spread_bias()
+            elif s == 2:
+                spread_gain()
             if s - 1 < n_chunks:
                 project(s - 1)
                 add_bias(s - 1)

@@ -32,7 +32,8 @@ HEAD_CHUNKS = 5
 BY_HEAD_CHUNKS = 2
 LAST_VECTOR_HEADS = 1
 POOL_HEADS = 3
-SCALAR_COPY_BANKS = (1, 2)
+TAIL_POOL_HEADS = 2
+SCALAR_COPY_BANKS = 1
 
 FLOPS = 2 * BATCH * TOKENS * K * FEATURES
 
@@ -57,6 +58,7 @@ def tile_ufoattention_pb_t_kernel(tc, queries, Wq_words, Wq_scales, bq, gamma, o
     nc = tc.nc
     chunks = chunk_list()
     n_chunks = len(chunks)
+    last = n_chunks - 1
     with ExitStack() as ctx:
         ctx.enter_context(tc.manual_schedule())
         consts = ctx.enter_context(tc.tile_pool(name="consts", bufs=1))
@@ -80,9 +82,14 @@ def tile_ufoattention_pb_t_kernel(tc, queries, Wq_words, Wq_scales, bq, gamma, o
             )
             x_tiles[c] = x_sb
 
+        ident = consts.tile([P, P], F32)
+        make_identity(nc, ident[:])
         bias_row = consts.tile([P, FEATURES], BF16)
         nc.vector.memset(bias_row[:], 0.0)
-        nc.scalar.dma_start(out=bias_row[0:1, :], in_=bq.rearrange("(a n) -> a n", a=1))
+        gain_row = consts.tile([P, HEADS], BF16)
+        nc.vector.memset(gain_row[:], 0.0)
+        nc.gpsimd.dma_start(out=bias_row[0:1, :], in_=bq.rearrange("(a n) -> a n", a=1))
+        nc.gpsimd.dma_start(out=gain_row[0:1, :], in_=gamma.rearrange("a h b c -> a (h b c)"))
         load(0)
         load(1)
 
@@ -95,19 +102,12 @@ def tile_ufoattention_pb_t_kernel(tc, queries, Wq_words, Wq_scales, bq, gamma, o
                 out=w_scales[32 * quad : 32 * quad + 4, :].bitcast(I32),
                 in_=Wq_scales[0, 4 * quad : 4 * quad + 4, :].bitcast(I32),
             )
-        load(2)
-        gain_row = consts.tile([P, HEADS], BF16)
-        nc.vector.memset(gain_row[:], 0.0)
-        nc.sync.dma_start(out=gain_row[0:1, :], in_=gamma.rearrange("a h b c -> a (h b c)"))
-        for c in range(3, AHEAD + 1):
+        for c in range(2, AHEAD + 1):
             load(c)
 
         one = consts.tile([P, 1], F32)
         nc.vector.memset(one[:], 1.0)
         nc.scalar.activation(out=one[:], in_=one[:], func=RSQRT)
-
-        ident = consts.tile([P, P], F32)
-        make_identity(nc, ident[:])
 
         ones = consts.tile([P, P], BF16)
         nc.vector.memset(ones[:], 1.0)
@@ -125,7 +125,7 @@ def tile_ufoattention_pb_t_kernel(tc, queries, Wq_words, Wq_scales, bq, gamma, o
                         nc.tensor.transpose(
                             xt[:, i, u, :], x_words[:, j * WORDS + u : (j + 1) * WORDS : 2], ident[:]
                         )
-                on_scalar = c < HEAD_CHUNKS or bank < SCALAR_COPY_BANKS[c % 2]
+                on_scalar = c < HEAD_CHUNKS or bank < SCALAR_COPY_BANKS
                 copy = nc.scalar.copy if on_scalar else nc.vector.tensor_copy
                 copy(
                     out=grouped_words[:, bank * PER_BANK : (bank + 1) * PER_BANK, :, :],
@@ -228,6 +228,11 @@ def tile_ufoattention_pb_t_kernel(tc, queries, Wq_words, Wq_scales, bq, gamma, o
                 in_=q_tiles[c][:, h, :, :].rearrange("p j d -> p (j d)"),
             )
 
+        def pool_heads(c):
+            if c < len(HEAD_SUBS):
+                return HEADS
+            return TAIL_POOL_HEADS if c == first_by_head - 1 else POOL_HEADS
+
         def factors_and_gpsimd(c):
             sub = chunks[c][2]
             q_sb = q_tiles[c]
@@ -239,21 +244,22 @@ def tile_ufoattention_pb_t_kernel(tc, queries, Wq_words, Wq_scales, bq, gamma, o
                 op=MULT,
             )
             factor_tiles[c] = factor
+            heads = pool_heads(c)
             nc.gpsimd.tensor_tensor(
-                out=q_sb[:, 0:POOL_HEADS, :, :],
-                in0=q_sb[:, 0:POOL_HEADS, :, :],
-                in1=factor[:, 0:POOL_HEADS, :, :].to_broadcast([P, POOL_HEADS, sub, HEAD_DIM]),
+                out=q_sb[:, 0:heads, :, :],
+                in0=q_sb[:, 0:heads, :, :],
+                in1=factor[:, 0:heads, :, :].to_broadcast([P, heads, sub, HEAD_DIM]),
                 op=MULT,
             )
             batch, first, sub = chunks[c]
             nc.sync.dma_start(
-                out=out[batch, 0:POOL_HEADS, first : first + P * sub, :].rearrange("h (p j) d -> p h (j d)", j=sub),
-                in_=q_sb[:, 0:POOL_HEADS, :, :].rearrange("p h j d -> p h (j d)"),
+                out=out[batch, 0:heads, first : first + P * sub, :].rearrange("h (p j) d -> p h (j d)", j=sub),
+                in_=q_sb[:, 0:heads, :, :].rearrange("p h j d -> p h (j d)"),
             )
 
         def scale_on_scalar(c):
             q_sb, factor = q_tiles[c], factor_tiles[c]
-            for h in range(POOL_HEADS, HEADS):
+            for h in range(pool_heads(c), HEADS):
                 for j in range(chunks[c][2]):
                     nc.scalar.activation(out=q_sb[:, h, j, :], in_=q_sb[:, h, j, :], func=COPY, scale=factor[:, h, j, :])
                 store(c, h)
@@ -287,23 +293,17 @@ def tile_ufoattention_pb_t_kernel(tc, queries, Wq_words, Wq_scales, bq, gamma, o
             nc.tensor.matmul(out=spread[:, 0, 0:HEADS], lhsT=ones[:], rhs=gain_row[:], start=True, stop=True)
             nc.vector.tensor_copy(out=gain[:].rearrange("p h o -> p (h o)"), in_=spread[:, 0, 0:HEADS])
 
-        last = n_chunks - 1
         first_by_head = n_chunks - BY_HEAD_CHUNKS
-        first_without_gpsimd = first_by_head - 2
         for s in range(1, n_chunks + 2):
-            late = s - 4
+            late = s - 3
             if s + AHEAD < n_chunks:
                 load(s + AHEAD)
             if s - 1 < n_chunks:
                 quantise(s - 1)
-            if 0 <= late < first_without_gpsimd:
+            if 0 <= late < first_by_head:
                 factors_and_gpsimd(late)
-            elif late == first_without_gpsimd:
-                scale_on_vector(late, range(HEADS))
             if s < n_chunks:
                 transpose_and_group(s)
-            if 0 <= s - 3 < first_by_head:
-                inverse_norms(s - 3)
             if s == 1:
                 spread_bias()
             elif s == 2:
@@ -311,12 +311,13 @@ def tile_ufoattention_pb_t_kernel(tc, queries, Wq_words, Wq_scales, bq, gamma, o
             if s - 1 < n_chunks:
                 project(s - 1)
                 add_bias(s - 1)
-            if s - 1 == last:
-                last_sums_on_vector(last)
-                scale_on_vector(first_by_head - 1, range(HEADS))
             if 0 <= s - 2 < first_by_head:
                 sum_squares(s - 2)
-                if 0 <= late < first_without_gpsimd:
+                if 0 <= late:
                     scale_on_scalar(late)
+                inverse_norms(s - 2)
             elif first_by_head <= s - 2:
+                if s == n_chunks:
+                    scale_on_vector(late, range(pool_heads(late), HEADS))
+                    last_sums_on_vector(last)
                 norms_and_scaling_by_head(s - 2)

@@ -12,7 +12,6 @@ FP8X4 = mybir.dt.float8_e4m3fn_x4
 FP4X4 = mybir.dt.float4_e2m1fn_x4
 ADD = mybir.AluOpType.add
 MULT = mybir.AluOpType.mult
-X_AXIS = mybir.AxisListType.X
 SQUARE = mybir.ActivationFunctionType.Square
 RSQRT = mybir.ActivationFunctionType.Abs_reciprocal_sqrt
 COPY = mybir.ActivationFunctionType.Copy
@@ -25,13 +24,13 @@ WORDS = K // 2
 SUB = 8
 PER_BANK = 2
 BANKS = SUB // PER_BANK
-AHEAD = 6
+AHEAD = 4
 HEAD_SUBS = [2, 2, 4]
 TAIL_SUBS = []
 HEAD_CHUNKS = 5
 BY_HEAD_CHUNKS = 2
-LAST_VECTOR_HEADS = 1
 POOL_HEADS = 3
+POOL_EXTRA = 1
 TAIL_POOL_HEADS = 2
 SCALAR_COPY_BANKS = 1
 
@@ -65,9 +64,9 @@ def tile_ufoattention_pb_t_kernel(tc, queries, Wq_words, Wq_scales, bq, gamma, o
         x_pool = ctx.enter_context(tc.tile_pool(name="x", bufs=AHEAD + 1))
         grouped_pool = ctx.enter_context(tc.tile_pool(name="grouped", bufs=2))
         mx_pool = ctx.enter_context(tc.tile_pool(name="mx", bufs=2))
-        q_pool = ctx.enter_context(tc.tile_pool(name="q", bufs=8))
-        squares_pool = ctx.enter_context(tc.tile_pool(name="squares", bufs=2))
-        stats_pool = ctx.enter_context(tc.tile_pool(name="stats", bufs=3))
+        q_pool = ctx.enter_context(tc.tile_pool(name="q", bufs=n_chunks))
+        squares_pool = ctx.enter_context(tc.tile_pool(name="squares", bufs=1))
+        stats_pool = ctx.enter_context(tc.tile_pool(name="stats", bufs=n_chunks))
         xt_pool = ctx.enter_context(tc.psum_pool(name="xt", bufs=BANKS))
         y_pool = ctx.enter_context(tc.psum_pool(name="y", bufs=BANKS))
 
@@ -86,10 +85,7 @@ def tile_ufoattention_pb_t_kernel(tc, queries, Wq_words, Wq_scales, bq, gamma, o
         make_identity(nc, ident[:])
         bias_row = consts.tile([P, FEATURES], BF16)
         nc.vector.memset(bias_row[:], 0.0)
-        gain_row = consts.tile([P, HEADS], BF16)
-        nc.vector.memset(gain_row[:], 0.0)
-        nc.gpsimd.dma_start(out=bias_row[0:1, :], in_=bq.rearrange("(a n) -> a n", a=1))
-        nc.gpsimd.dma_start(out=gain_row[0:1, :], in_=gamma.rearrange("a h b c -> a (h b c)"))
+        nc.scalar.dma_start(out=bias_row[0:1, :], in_=bq.rearrange("(a n) -> a n", a=1))
         load(0)
         load(1)
 
@@ -102,7 +98,11 @@ def tile_ufoattention_pb_t_kernel(tc, queries, Wq_words, Wq_scales, bq, gamma, o
                 out=w_scales[32 * quad : 32 * quad + 4, :].bitcast(I32),
                 in_=Wq_scales[0, 4 * quad : 4 * quad + 4, :].bitcast(I32),
             )
-        for c in range(2, AHEAD + 1):
+        load(2)
+        gain_row = consts.tile([P, HEADS], BF16)
+        nc.vector.memset(gain_row[:], 0.0)
+        nc.sync.dma_start(out=gain_row[0:1, :], in_=gamma.rearrange("a h b c -> a (h b c)"))
+        for c in range(3, AHEAD + 1):
             load(c)
 
         one = consts.tile([P, 1], F32)
@@ -183,31 +183,15 @@ def tile_ufoattention_pb_t_kernel(tc, queries, Wq_words, Wq_scales, bq, gamma, o
                     )
             sum_tiles[c] = sums
 
-        def last_sums_on_vector(c):
-            sub = chunks[c][2]
-            q_part = q_tiles[c][:, HEADS - LAST_VECTOR_HEADS :, :, :]
-            sums = stats_pool.tile([P, HEADS, sub], F32)
-            products = squares_pool.tile([P, LAST_VECTOR_HEADS, sub, HEAD_DIM], F32)
-            nc.vector.tensor_tensor(out=products[:], in0=q_part, in1=q_part, op=MULT)
-            nc.vector.tensor_reduce(out=sums[:, HEADS - LAST_VECTOR_HEADS :, :], in_=products[:], axis=X_AXIS, op=ADD)
-            sum_tiles[c] = sums
-
         def norms_and_scaling_by_head(c):
             sub = chunks[c][2]
             q_sb = q_tiles[c]
             squares = squares_pool.tile([P, HEADS, sub, HEAD_DIM], F32)
             inverse = stats_pool.tile([P, HEADS, sub], F32)
             inverse_tiles[c] = inverse
-            by_scalar = HEADS
-            if c in sum_tiles:
-                sums = sum_tiles[c]
-                by_scalar = HEADS - LAST_VECTOR_HEADS
-                nc.scalar.activation(out=inverse[:, by_scalar:, :], in_=sums[:, by_scalar:, :], func=RSQRT)
-                scale_on_vector(c, range(by_scalar, HEADS))
-            else:
-                sums = stats_pool.tile([P, HEADS, sub], F32)
-            for h in range(by_scalar + 1):
-                if h < by_scalar:
+            sums = stats_pool.tile([P, HEADS, sub], F32)
+            for h in range(HEADS + 1):
+                if h < HEADS:
                     for j in range(sub):
                         nc.scalar.activation(
                             out=squares[:, h, j, :], in_=q_sb[:, h, j, :], func=SQUARE, accum_out=sums[:, h, j : j + 1]
@@ -228,10 +212,10 @@ def tile_ufoattention_pb_t_kernel(tc, queries, Wq_words, Wq_scales, bq, gamma, o
                 in_=q_tiles[c][:, h, :, :].rearrange("p j d -> p (j d)"),
             )
 
-        def pool_heads(c):
+        def pool_share(c):
             if c < len(HEAD_SUBS):
-                return HEADS
-            return TAIL_POOL_HEADS if c == first_by_head - 1 else POOL_HEADS
+                return HEADS, 0
+            return (TAIL_POOL_HEADS, 0) if c == first_by_head - 1 else (POOL_HEADS, POOL_EXTRA)
 
         def factors_and_gpsimd(c):
             sub = chunks[c][2]
@@ -244,11 +228,13 @@ def tile_ufoattention_pb_t_kernel(tc, queries, Wq_words, Wq_scales, bq, gamma, o
                 op=MULT,
             )
             factor_tiles[c] = factor
-            heads = pool_heads(c)
+            heads, extra = pool_share(c)
+            rows = heads * sub + extra
+            q_rows = q_sb[:].rearrange("p h j d -> p (h j) d")
             nc.gpsimd.tensor_tensor(
-                out=q_sb[:, 0:heads, :, :],
-                in0=q_sb[:, 0:heads, :, :],
-                in1=factor[:, 0:heads, :, :].to_broadcast([P, heads, sub, HEAD_DIM]),
+                out=q_rows[:, 0:rows, :],
+                in0=q_rows[:, 0:rows, :],
+                in1=factor[:].rearrange("p h j o -> p (h j) o")[:, 0:rows, :].to_broadcast([P, rows, HEAD_DIM]),
                 op=MULT,
             )
             batch, first, sub = chunks[c]
@@ -259,8 +245,9 @@ def tile_ufoattention_pb_t_kernel(tc, queries, Wq_words, Wq_scales, bq, gamma, o
 
         def scale_on_scalar(c):
             q_sb, factor = q_tiles[c], factor_tiles[c]
-            for h in range(pool_heads(c), HEADS):
-                for j in range(chunks[c][2]):
+            heads, extra = pool_share(c)
+            for h in range(heads, HEADS):
+                for j in range(extra if h == heads else 0, chunks[c][2]):
                     nc.scalar.activation(out=q_sb[:, h, j, :], in_=q_sb[:, h, j, :], func=COPY, scale=factor[:, h, j, :])
                 store(c, h)
 
@@ -318,6 +305,5 @@ def tile_ufoattention_pb_t_kernel(tc, queries, Wq_words, Wq_scales, bq, gamma, o
                 inverse_norms(s - 2)
             elif first_by_head <= s - 2:
                 if s == n_chunks:
-                    scale_on_vector(late, range(pool_heads(late), HEADS))
-                    last_sums_on_vector(last)
+                    scale_on_vector(late, range(pool_share(late)[0], HEADS))
                 norms_and_scaling_by_head(s - 2)

@@ -32,7 +32,7 @@ BY_HEAD_CHUNKS = 2
 POOL_HEADS = 3
 POOL_EXTRA = 1
 TAIL_POOL_HEADS = 2
-SCALAR_COPY_BANKS = 1
+SCALAR_COPY_BANKS = (1, 2)
 
 FLOPS = 2 * BATCH * TOKENS * K * FEATURES
 
@@ -125,7 +125,7 @@ def tile_ufoattention_pb_t_kernel(tc, queries, Wq_words, Wq_scales, bq, gamma, o
                         nc.tensor.transpose(
                             xt[:, i, u, :], x_words[:, j * WORDS + u : (j + 1) * WORDS : 2], ident[:]
                         )
-                on_scalar = c < HEAD_CHUNKS or bank < SCALAR_COPY_BANKS
+                on_scalar = c < HEAD_CHUNKS or bank < SCALAR_COPY_BANKS[c % 2]
                 copy = nc.scalar.copy if on_scalar else nc.vector.tensor_copy
                 copy(
                     out=grouped_words[:, bank * PER_BANK : (bank + 1) * PER_BANK, :, :],

@@ -30,9 +30,9 @@ TAIL_SUBS = []
 HEAD_CHUNKS = 5
 BY_HEAD_CHUNKS = 2
 POOL_HEADS = 3
-POOL_EXTRA = 1
-TAIL_POOL_HEADS = 2
-SCALAR_COPY_BANKS = (1, 2)
+TAIL_POOL_HEADS = 1
+TAIL_VECTOR_HEADS = 2
+SCALAR_COPY_BANKS = (1, 1, 2)
 
 FLOPS = 2 * BATCH * TOKENS * K * FEATURES
 
@@ -125,7 +125,7 @@ def tile_ufoattention_pb_t_kernel(tc, queries, Wq_words, Wq_scales, bq, gamma, o
                         nc.tensor.transpose(
                             xt[:, i, u, :], x_words[:, j * WORDS + u : (j + 1) * WORDS : 2], ident[:]
                         )
-                on_scalar = c < HEAD_CHUNKS or bank < SCALAR_COPY_BANKS[c % 2]
+                on_scalar = c < HEAD_CHUNKS or bank < SCALAR_COPY_BANKS[c % len(SCALAR_COPY_BANKS)]
                 copy = nc.scalar.copy if on_scalar else nc.vector.tensor_copy
                 copy(
                     out=grouped_words[:, bank * PER_BANK : (bank + 1) * PER_BANK, :, :],
@@ -212,10 +212,10 @@ def tile_ufoattention_pb_t_kernel(tc, queries, Wq_words, Wq_scales, bq, gamma, o
                 in_=q_tiles[c][:, h, :, :].rearrange("p j d -> p (j d)"),
             )
 
-        def pool_share(c):
+        def pool_heads(c):
             if c < len(HEAD_SUBS):
-                return HEADS, 0
-            return (TAIL_POOL_HEADS, 0) if c == first_by_head - 1 else (POOL_HEADS, POOL_EXTRA)
+                return HEADS
+            return TAIL_POOL_HEADS if c == first_by_head - 1 else POOL_HEADS
 
         def factors_and_gpsimd(c):
             sub = chunks[c][2]
@@ -228,13 +228,11 @@ def tile_ufoattention_pb_t_kernel(tc, queries, Wq_words, Wq_scales, bq, gamma, o
                 op=MULT,
             )
             factor_tiles[c] = factor
-            heads, extra = pool_share(c)
-            rows = heads * sub + extra
-            q_rows = q_sb[:].rearrange("p h j d -> p (h j) d")
+            heads = pool_heads(c)
             nc.gpsimd.tensor_tensor(
-                out=q_rows[:, 0:rows, :],
-                in0=q_rows[:, 0:rows, :],
-                in1=factor[:].rearrange("p h j o -> p (h j) o")[:, 0:rows, :].to_broadcast([P, rows, HEAD_DIM]),
+                out=q_sb[:, 0:heads, :, :],
+                in0=q_sb[:, 0:heads, :, :],
+                in1=factor[:, 0:heads, :, :].to_broadcast([P, heads, sub, HEAD_DIM]),
                 op=MULT,
             )
             batch, first, sub = chunks[c]
@@ -245,9 +243,8 @@ def tile_ufoattention_pb_t_kernel(tc, queries, Wq_words, Wq_scales, bq, gamma, o
 
         def scale_on_scalar(c):
             q_sb, factor = q_tiles[c], factor_tiles[c]
-            heads, extra = pool_share(c)
-            for h in range(heads, HEADS):
-                for j in range(extra if h == heads else 0, chunks[c][2]):
+            for h in range(pool_heads(c), HEADS):
+                for j in range(chunks[c][2]):
                     nc.scalar.activation(out=q_sb[:, h, j, :], in_=q_sb[:, h, j, :], func=COPY, scale=factor[:, h, j, :])
                 store(c, h)
 
@@ -287,6 +284,8 @@ def tile_ufoattention_pb_t_kernel(tc, queries, Wq_words, Wq_scales, bq, gamma, o
                 load(s + AHEAD)
             if s - 1 < n_chunks:
                 quantise(s - 1)
+            if s == n_chunks:
+                scale_on_vector(late, range(HEADS - TAIL_VECTOR_HEADS, HEADS))
             if 0 <= late < first_by_head:
                 factors_and_gpsimd(late)
             if s < n_chunks:
@@ -305,5 +304,5 @@ def tile_ufoattention_pb_t_kernel(tc, queries, Wq_words, Wq_scales, bq, gamma, o
                 inverse_norms(s - 2)
             elif first_by_head <= s - 2:
                 if s == n_chunks:
-                    scale_on_vector(late, range(pool_share(late)[0], HEADS))
+                    scale_on_vector(late, range(pool_heads(late), HEADS - TAIL_VECTOR_HEADS))
                 norms_and_scaling_by_head(s - 2)

@@ -30,9 +30,10 @@ TAIL_SUBS = []
 HEAD_CHUNKS = 5
 BY_HEAD_CHUNKS = 2
 POOL_HEADS = 3
+POOL_EXTRA = 2
 TAIL_POOL_HEADS = 1
 TAIL_VECTOR_HEADS = 2
-SCALAR_COPY_BANKS = (1, 1, 2)
+SCALAR_SUBS = 3
 
 FLOPS = 2 * BATCH * TOKENS * K * FEATURES
 
@@ -70,7 +71,7 @@ def tile_ufoattention_pb_t_kernel(tc, queries, Wq_words, Wq_scales, bq, gamma, o
         xt_pool = ctx.enter_context(tc.psum_pool(name="xt", bufs=BANKS))
         y_pool = ctx.enter_context(tc.psum_pool(name="y", bufs=BANKS))
 
-        x_tiles, grouped_tiles, code_tiles, plane_tiles = {}, {}, {}, {}
+        x_tiles, xt_tiles, grouped_tiles, code_tiles, plane_tiles = {}, {}, {}, {}, {}
         y_tiles, q_tiles, sum_tiles, inverse_tiles, factor_tiles = {}, {}, {}, {}, {}
 
         def load(c):
@@ -112,26 +113,42 @@ def tile_ufoattention_pb_t_kernel(tc, queries, Wq_words, Wq_scales, bq, gamma, o
         ones = consts.tile([P, P], BF16)
         nc.vector.memset(ones[:], 1.0)
 
-        def transpose_and_group(c):
-            sub = chunks[c][2]
+        def transpose(c):
             x_words = x_tiles[c][:].bitcast(F32)
-            grouped = grouped_pool.tile([P, sub * P * 4], BF16, align_bytes=64)
-            grouped_words = grouped[:].bitcast(F32).rearrange("p (j c u) -> p j c u", j=sub, u=2)
+            for j in range(chunks[c][2]):
+                if j % PER_BANK == 0:
+                    xt = xt_pool.tile([P, PER_BANK, 2, P], F32)
+                    xt_tiles[c, j // PER_BANK] = xt
+                for u in range(2):
+                    nc.tensor.transpose(
+                        xt[:, j % PER_BANK, u, :], x_words[:, j * WORDS + u : (j + 1) * WORDS : 2], ident[:]
+                    )
+
+        def scalar_subs(c):
+            sub = chunks[c][2]
+            if c < len(HEAD_SUBS):
+                return range(sub)
+            return range(sub - PER_BANK) if c < HEAD_CHUNKS else range(sub - SCALAR_SUBS, sub)
+
+        def group(c, copy, subs):
+            sub = chunks[c][2]
+            if c not in grouped_tiles:
+                grouped_tiles[c] = grouped_pool.tile([P, sub * P * 4], BF16, align_bytes=64, name="grouped")
+            grouped_words = grouped_tiles[c][:].bitcast(F32).rearrange("p (j c u) -> p j c u", j=sub, u=2)
             for bank in range(sub // PER_BANK):
-                xt = xt_pool.tile([P, PER_BANK, 2, P], F32)
-                for i in range(PER_BANK):
-                    j = bank * PER_BANK + i
-                    for u in range(2):
-                        nc.tensor.transpose(
-                            xt[:, i, u, :], x_words[:, j * WORDS + u : (j + 1) * WORDS : 2], ident[:]
-                        )
-                on_scalar = c < HEAD_CHUNKS or bank < SCALAR_COPY_BANKS[c % len(SCALAR_COPY_BANKS)]
-                copy = nc.scalar.copy if on_scalar else nc.vector.tensor_copy
-                copy(
-                    out=grouped_words[:, bank * PER_BANK : (bank + 1) * PER_BANK, :, :],
-                    in_=xt[:].rearrange("p i u c -> p i c u"),
-                )
-            grouped_tiles[c] = grouped
+                mine = [i for i in range(PER_BANK) if bank * PER_BANK + i in subs]
+                if mine:
+                    first, end = mine[0], mine[-1] + 1
+                    copy(
+                        out=grouped_words[:, bank * PER_BANK + first : bank * PER_BANK + end, :, :],
+                        in_=xt_tiles[c, bank][:, first:end, :, :].rearrange("p i u c -> p i c u"),
+                    )
+
+        def group_on_scalar(c):
+            group(c, nc.scalar.copy, scalar_subs(c))
+
+        def group_on_vector(c):
+            group(c, nc.vector.tensor_copy, [j for j in range(chunks[c][2]) if j not in scalar_subs(c)])
 
         def quantise(c):
             sub = chunks[c][2]
@@ -212,10 +229,12 @@ def tile_ufoattention_pb_t_kernel(tc, queries, Wq_words, Wq_scales, bq, gamma, o
                 in_=q_tiles[c][:, h, :, :].rearrange("p j d -> p (j d)"),
             )
 
-        def pool_heads(c):
+        def pool_share(c):
             if c < len(HEAD_SUBS):
-                return HEADS
-            return TAIL_POOL_HEADS if c == first_by_head - 1 else POOL_HEADS
+                return HEADS, 0
+            if c >= first_by_head - 2:
+                return (POOL_HEADS, 0) if c == first_by_head - 2 else (TAIL_POOL_HEADS, 0)
+            return POOL_HEADS, POOL_EXTRA
 
         def factors_and_gpsimd(c):
             sub = chunks[c][2]
@@ -228,11 +247,13 @@ def tile_ufoattention_pb_t_kernel(tc, queries, Wq_words, Wq_scales, bq, gamma, o
                 op=MULT,
             )
             factor_tiles[c] = factor
-            heads = pool_heads(c)
+            heads, extra = pool_share(c)
+            rows = heads * sub + extra
+            q_rows = q_sb[:].rearrange("p h j d -> p (h j) d")
             nc.gpsimd.tensor_tensor(
-                out=q_sb[:, 0:heads, :, :],
-                in0=q_sb[:, 0:heads, :, :],
-                in1=factor[:, 0:heads, :, :].to_broadcast([P, heads, sub, HEAD_DIM]),
+                out=q_rows[:, 0:rows, :],
+                in0=q_rows[:, 0:rows, :],
+                in1=factor[:].rearrange("p h j o -> p (h j) o")[:, 0:rows, :].to_broadcast([P, rows, HEAD_DIM]),
                 op=MULT,
             )
             batch, first, sub = chunks[c]
@@ -243,8 +264,9 @@ def tile_ufoattention_pb_t_kernel(tc, queries, Wq_words, Wq_scales, bq, gamma, o
 
         def scale_on_scalar(c):
             q_sb, factor = q_tiles[c], factor_tiles[c]
-            for h in range(pool_heads(c), HEADS):
-                for j in range(chunks[c][2]):
+            heads, extra = pool_share(c)
+            for h in range(heads, HEADS):
+                for j in range(extra if h == heads else 0, chunks[c][2]):
                     nc.scalar.activation(out=q_sb[:, h, j, :], in_=q_sb[:, h, j, :], func=COPY, scale=factor[:, h, j, :])
                 store(c, h)
 
@@ -262,7 +284,8 @@ def tile_ufoattention_pb_t_kernel(tc, queries, Wq_words, Wq_scales, bq, gamma, o
                     )
                 store(c, h)
 
-        transpose_and_group(0)
+        transpose(0)
+        group_on_scalar(0)
 
         bias = consts.tile([P, PER_BANK, FEATURES], F32)
         gain = consts.tile([P, HEADS, 1], F32)
@@ -282,14 +305,18 @@ def tile_ufoattention_pb_t_kernel(tc, queries, Wq_words, Wq_scales, bq, gamma, o
             late = s - 3
             if s + AHEAD < n_chunks:
                 load(s + AHEAD)
+            if 0 <= late and s < n_chunks:
+                factors_and_gpsimd(late)
             if s - 1 < n_chunks:
                 quantise(s - 1)
             if s == n_chunks:
                 scale_on_vector(late, range(HEADS - TAIL_VECTOR_HEADS, HEADS))
-            if 0 <= late < first_by_head:
                 factors_and_gpsimd(late)
             if s < n_chunks:
-                transpose_and_group(s)
+                transpose(s)
+                if s < HEAD_CHUNKS:
+                    group_on_scalar(s)
+                group_on_vector(s)
             if s == 1:
                 spread_bias()
             elif s == 2:
@@ -299,10 +326,12 @@ def tile_ufoattention_pb_t_kernel(tc, queries, Wq_words, Wq_scales, bq, gamma, o
                 add_bias(s - 1)
             if 0 <= s - 2 < first_by_head:
                 sum_squares(s - 2)
+                if HEAD_CHUNKS <= s < n_chunks:
+                    group_on_scalar(s)
                 if 0 <= late:
                     scale_on_scalar(late)
                 inverse_norms(s - 2)
             elif first_by_head <= s - 2:
                 if s == n_chunks:
-                    scale_on_vector(late, range(pool_heads(late), HEADS - TAIL_VECTOR_HEADS))
+                    scale_on_vector(late, range(TAIL_POOL_HEADS, HEADS - TAIL_VECTOR_HEADS))
                 norms_and_scaling_by_head(s - 2)

from contextlib import ExitStack

import concourse.mybir as mybir
from concourse.masks import make_identity

F32 = mybir.dt.float32
BF16 = mybir.dt.bfloat16
I32 = mybir.dt.int32
U32 = mybir.dt.uint32
U8 = mybir.dt.uint8
FP8X4 = mybir.dt.float8_e4m3fn_x4
FP4X4 = mybir.dt.float4_e2m1fn_x4
ADD = mybir.AluOpType.add
MULT = mybir.AluOpType.mult
SQUARE = mybir.ActivationFunctionType.Square
RSQRT = mybir.ActivationFunctionType.Abs_reciprocal_sqrt
COPY = mybir.ActivationFunctionType.Copy

P = 128
BATCH, TOKENS, K = 4, 4096, 512
HEADS, HEAD_DIM = 4, 64
FEATURES = HEADS * HEAD_DIM
WORDS = K // 2
SUB = 8
PER_BANK = 2
BANKS = SUB // PER_BANK
AHEAD = 4
HEAD_SUBS = [2, 2, 4]
TAIL_SUBS = []
HEAD_CHUNKS = 5
BY_HEAD_CHUNKS = 2
POOL_HEADS = 3
POOL_EXTRA = 2
TAIL_POOL_HEADS = 1
TAIL_VECTOR_HEADS = 2
SCALAR_SUBS = 3

FLOPS = 2 * BATCH * TOKENS * K * FEATURES


def chunk_list():
    chunks = []
    for batch in range(BATCH):
        subs = [SUB] * (TOKENS // (P * SUB))
        if batch == 0:
            subs = HEAD_SUBS + subs[sum(HEAD_SUBS) // SUB :]
        if batch == BATCH - 1:
            subs = subs[: len(subs) - sum(TAIL_SUBS) // SUB] + TAIL_SUBS
        first = 0
        for sub in subs:
            chunks.append((batch, first, sub))
            first += P * sub
        assert first == TOKENS
    return chunks


def tile_ufoattention_pb_t_kernel(tc, queries, Wq_words, Wq_scales, bq, gamma, out):
    nc = tc.nc
    chunks = chunk_list()
    n_chunks = len(chunks)
    last = n_chunks - 1
    with ExitStack() as ctx:
        ctx.enter_context(tc.manual_schedule())
        consts = ctx.enter_context(tc.tile_pool(name="consts", bufs=1))
        x_pool = ctx.enter_context(tc.tile_pool(name="x", bufs=AHEAD + 1))
        grouped_pool = ctx.enter_context(tc.tile_pool(name="grouped", bufs=2))
        mx_pool = ctx.enter_context(tc.tile_pool(name="mx", bufs=2))
        q_pool = ctx.enter_context(tc.tile_pool(name="q", bufs=n_chunks))
        squares_pool = ctx.enter_context(tc.tile_pool(name="squares", bufs=1))
        stats_pool = ctx.enter_context(tc.tile_pool(name="stats", bufs=n_chunks))
        xt_pool = ctx.enter_context(tc.psum_pool(name="xt", bufs=BANKS))
        y_pool = ctx.enter_context(tc.psum_pool(name="y", bufs=BANKS))

        x_tiles, xt_tiles, grouped_tiles, code_tiles, plane_tiles = {}, {}, {}, {}, {}
        y_tiles, q_tiles, sum_tiles, inverse_tiles, factor_tiles = {}, {}, {}, {}, {}

        def load(c):
            batch, first, sub = chunks[c]
            x_sb = x_pool.tile([P, sub * K], BF16)
            nc.sync.dma_start(
                out=x_sb[:], in_=queries[batch, first : first + P * sub, :].rearrange("(p j) k -> p (j k)", j=sub)
            )
            x_tiles[c] = x_sb

        ident = consts.tile([P, P], F32)
        make_identity(nc, ident[:])
        bias_row = consts.tile([P, FEATURES], BF16)
        nc.vector.memset(bias_row[:], 0.0)
        nc.scalar.dma_start(out=bias_row[0:1, :], in_=bq.rearrange("(a n) -> a n", a=1))
        load(0)
        load(1)

        w_words = consts.tile([P, 2 * FEATURES], U8, align_bytes=64)
        nc.sync.dma_start(out=w_words[:].bitcast(I32), in_=Wq_words[0].bitcast(I32))
        w_scales = consts.tile([P, FEATURES], U8, align_bytes=64)
        nc.vector.memset(w_scales[:].bitcast(I32), 0)
        for quad in range(4):
            nc.sync.dma_start(
                out=w_scales[32 * quad : 32 * quad + 4, :].bitcast(I32),
                in_=Wq_scales[0, 4 * quad : 4 * quad + 4, :].bitcast(I32),
            )
        load(2)
        gain_row = consts.tile([P, HEADS], BF16)
        nc.vector.memset(gain_row[:], 0.0)
        nc.sync.dma_start(out=gain_row[0:1, :], in_=gamma.rearrange("a h b c -> a (h b c)"))
        for c in range(3, AHEAD + 1):
            load(c)

        one = consts.tile([P, 1], F32)
        nc.vector.memset(one[:], 1.0)
        nc.scalar.activation(out=one[:], in_=one[:], func=RSQRT)

        ones = consts.tile([P, P], BF16)
        nc.vector.memset(ones[:], 1.0)

        def transpose(c):
            x_words = x_tiles[c][:].bitcast(F32)
            for j in range(chunks[c][2]):
                if j % PER_BANK == 0:
                    xt = xt_pool.tile([P, PER_BANK, 2, P], F32)
                    xt_tiles[c, j // PER_BANK] = xt
                for u in range(2):
                    nc.tensor.transpose(
                        xt[:, j % PER_BANK, u, :], x_words[:, j * WORDS + u : (j + 1) * WORDS : 2], ident[:]
                    )

        def scalar_subs(c):
            sub = chunks[c][2]
            if c < len(HEAD_SUBS):
                return range(sub)
            return range(sub - PER_BANK) if c < HEAD_CHUNKS else range(sub - SCALAR_SUBS, sub)

        def group(c, copy, subs):
            sub = chunks[c][2]
            if c not in grouped_tiles:
                grouped_tiles[c] = grouped_pool.tile([P, sub * P * 4], BF16, align_bytes=64, name="grouped")
            grouped_words = grouped_tiles[c][:].bitcast(F32).rearrange("p (j c u) -> p j c u", j=sub, u=2)
            for bank in range(sub // PER_BANK):
                mine = [i for i in range(PER_BANK) if bank * PER_BANK + i in subs]
                if mine:
                    first, end = mine[0], mine[-1] + 1
                    copy(
                        out=grouped_words[:, bank * PER_BANK + first : bank * PER_BANK + end, :, :],
                        in_=xt_tiles[c, bank][:, first:end, :, :].rearrange("p i u c -> p i c u"),
                    )

        def group_on_scalar(c):
            group(c, nc.scalar.copy, scalar_subs(c))

        def group_on_vector(c):
            group(c, nc.vector.tensor_copy, [j for j in range(chunks[c][2]) if j not in scalar_subs(c)])

        def quantise(c):
            sub = chunks[c][2]
            codes = mx_pool.tile([P, sub * P], U32, align_bytes=64)
            planes = mx_pool.tile([P, sub * P], U8, align_bytes=64)
            nc.vector.quantize_mx(
                out=codes[:].bitcast(FP8X4), scales=planes[:], in_=grouped_tiles[c][:]
            )
            code_tiles[c], plane_tiles[c] = codes, planes

        def project(c):
            codes, planes = code_tiles[c], plane_tiles[c]
            y_tiles[c] = []
            for bank in range(chunks[c][2] // PER_BANK):
                y_ps = y_pool.tile([P, PER_BANK, FEATURES], F32)
                for i in range(PER_BANK):
                    cols = slice((bank * PER_BANK + i) * P, (bank * PER_BANK + i + 1) * P)
                    nc.tensor.matmul_mx(
                        out=y_ps[:, i, :],
                        lhsT=codes[:, cols].bitcast(FP8X4),
                        lhsT_scale=planes[:, cols],
                        rhs=w_words[:].bitcast(FP4X4),
                        rhs_scale=w_scales[:],
                        start=True,
                        stop=True,
                    )
                y_tiles[c].append(y_ps)

        def add_bias(c):
            q_sb = q_pool.tile([P, HEADS, chunks[c][2], HEAD_DIM], F32)
            for bank, y_ps in enumerate(y_tiles[c]):
                nc.vector.tensor_tensor(
                    out=q_sb[:, :, bank * PER_BANK : (bank + 1) * PER_BANK, :].rearrange("p h i d -> p i h d"),
                    in0=y_ps[:].rearrange("p i (h d) -> p i h d", h=HEADS),
                    in1=bias[:].rearrange("p i (h d) -> p i h d", h=HEADS),
                    op=ADD,
                )
            q_tiles[c] = q_sb

        def sum_squares(c):
            sub = chunks[c][2]
            q_sb = q_tiles[c]
            squares = squares_pool.tile([P, HEADS, sub, HEAD_DIM], F32)
            sums = stats_pool.tile([P, HEADS, sub], F32)
            for j in range(sub):
                for h in range(HEADS):
                    nc.scalar.activation(
                        out=squares[:, h, j, :], in_=q_sb[:, h, j, :], func=SQUARE, accum_out=sums[:, h, j : j + 1]
                    )
            sum_tiles[c] = sums

        def norms_and_scaling_by_head(c):
            sub = chunks[c][2]
            q_sb = q_tiles[c]
            squares = squares_pool.tile([P, HEADS, sub, HEAD_DIM], F32)
            inverse = stats_pool.tile([P, HEADS, sub], F32)
            inverse_tiles[c] = inverse
            sums = stats_pool.tile([P, HEADS, sub], F32)
            for h in range(HEADS + 1):
                if h < HEADS:
                    for j in range(sub):
                        nc.scalar.activation(
                            out=squares[:, h, j, :], in_=q_sb[:, h, j, :], func=SQUARE, accum_out=sums[:, h, j : j + 1]
                        )
                if h > 0:
                    nc.scalar.activation(out=inverse[:, h - 1, :], in_=sums[:, h - 1, :], func=RSQRT)
                    scale_on_vector(c, [h - 1])

        def inverse_norms(c):
            inverse = stats_pool.tile([P, HEADS, chunks[c][2]], F32)
            nc.scalar.activation(out=inverse[:], in_=sum_tiles[c][:], func=RSQRT)
            inverse_tiles[c] = inverse

        def store(c, h):
            batch, first, sub = chunks[c]
            nc.sync.dma_start(
                out=out[batch, h, first : first + P * sub, :].rearrange("(p j) d -> p (j d)", j=sub),
                in_=q_tiles[c][:, h, :, :].rearrange("p j d -> p (j d)"),
            )

        def pool_share(c):
            if c < len(HEAD_SUBS):
                return HEADS, 0
            if c >= first_by_head - 2:
                return (POOL_HEADS, 0) if c == first_by_head - 2 else (TAIL_POOL_HEADS, 0)
            return POOL_HEADS, POOL_EXTRA

        def factors_and_gpsimd(c):
            sub = chunks[c][2]
            q_sb = q_tiles[c]
            factor = stats_pool.tile([P, HEADS, sub, 1], F32)
            nc.vector.tensor_tensor(
                out=factor[:].rearrange("p h j o -> p h (j o)"),
                in0=inverse_tiles[c][:],
                in1=gain[:].to_broadcast([P, HEADS, sub]),
                op=MULT,
            )
            factor_tiles[c] = factor
            heads, extra = pool_share(c)
            rows = heads * sub + extra
            q_rows = q_sb[:].rearrange("p h j d -> p (h j) d")
            nc.gpsimd.tensor_tensor(
                out=q_rows[:, 0:rows, :],
                in0=q_rows[:, 0:rows, :],
                in1=factor[:].rearrange("p h j o -> p (h j) o")[:, 0:rows, :].to_broadcast([P, rows, HEAD_DIM]),
                op=MULT,
            )
            batch, first, sub = chunks[c]
            nc.sync.dma_start(
                out=out[batch, 0:heads, first : first + P * sub, :].rearrange("h (p j) d -> p h (j d)", j=sub),
                in_=q_sb[:, 0:heads, :, :].rearrange("p h j d -> p h (j d)"),
            )

        def scale_on_scalar(c):
            q_sb, factor = q_tiles[c], factor_tiles[c]
            heads, extra = pool_share(c)
            for h in range(heads, HEADS):
                for j in range(extra if h == heads else 0, chunks[c][2]):
                    nc.scalar.activation(out=q_sb[:, h, j, :], in_=q_sb[:, h, j, :], func=COPY, scale=factor[:, h, j, :])
                store(c, h)

        def scale_on_vector(c, heads):
            q_sb, inverse = q_tiles[c], inverse_tiles[c]
            for h in heads:
                for j in range(chunks[c][2]):
                    nc.vector.tensor_scalar(
                        out=q_sb[:, h, j, :],
                        in0=q_sb[:, h, j, :],
                        scalar1=inverse[:, h, j : j + 1],
                        scalar2=gain[:, h, :],
                        op0=MULT,
                        op1=MULT,
                    )
                store(c, h)

        transpose(0)
        group_on_scalar(0)

        bias = consts.tile([P, PER_BANK, FEATURES], F32)
        gain = consts.tile([P, HEADS, 1], F32)

        def spread_bias():
            spread = y_pool.tile([P, PER_BANK, FEATURES], F32, tag="y_ps")
            nc.tensor.matmul(out=spread[:, 0, :], lhsT=ones[:], rhs=bias_row[:], start=True, stop=True)
            nc.vector.tensor_copy(out=bias[:], in_=spread[:, 0:1, :].to_broadcast([P, PER_BANK, FEATURES]))

        def spread_gain():
            spread = y_pool.tile([P, PER_BANK, FEATURES], F32, tag="y_ps")
            nc.tensor.matmul(out=spread[:, 0, 0:HEADS], lhsT=ones[:], rhs=gain_row[:], start=True, stop=True)
            nc.vector.tensor_copy(out=gain[:].rearrange("p h o -> p (h o)"), in_=spread[:, 0, 0:HEADS])

        first_by_head = n_chunks - BY_HEAD_CHUNKS
        for s in range(1, n_chunks + 2):
            late = s - 3
            if s + AHEAD < n_chunks:
                load(s + AHEAD)
            if 0 <= late and s < n_chunks:
                factors_and_gpsimd(late)
            if s - 1 < n_chunks:
                quantise(s - 1)
            if s == n_chunks:
                scale_on_vector(late, range(HEADS - TAIL_VECTOR_HEADS, HEADS))
                factors_and_gpsimd(late)
            if s < n_chunks:
                transpose(s)
                if s < HEAD_CHUNKS:
                    group_on_scalar(s)
                group_on_vector(s)
            if s == 1:
                spread_bias()
            elif s == 2:
                spread_gain()
            if s - 1 < n_chunks:
                project(s - 1)
                add_bias(s - 1)
            if 0 <= s - 2 < first_by_head:
                sum_squares(s - 2)
                if HEAD_CHUNKS <= s < n_chunks:
                    group_on_scalar(s)
                if 0 <= late:
                    scale_on_scalar(late)
                inverse_norms(s - 2)
            elif first_by_head <= s - 2:
                if s == n_chunks:
                    scale_on_vector(late, range(TAIL_POOL_HEADS, HEADS - TAIL_VECTOR_HEADS))
                norms_and_scaling_by_head(s - 2)
